import numpy as np
import ml_dtypes


def mxq(x, axis, fmt="e4m3"):
    dtype, down = {"e4m3": (ml_dtypes.float8_e4m3fn, 7), "e5m2": (ml_dtypes.float8_e5m2, 14)}[fmt]
    v = np.moveaxis(np.asarray(x, np.float32).astype(ml_dtypes.bfloat16).astype(np.float64), axis, -1)
    blocks = v.reshape(v.shape[:-1] + (-1, 32))
    amax = np.abs(blocks).max(-1, keepdims=True)
    byte = np.maximum(np.where(amax > 0, np.frexp(amax)[1] - 1 + 127, 0) - down, 1)
    scale = np.exp2(byte - 127.0)
    codes = (blocks / scale).astype(np.float32).astype(dtype).astype(np.float64)
    return np.moveaxis((codes * scale).reshape(v.shape), -1, axis)


WIDE = False


def mx_kscale(k):
    if not WIDE:
        return np.ones(k)
    levels = np.array([10, -10, 5, -5, 0])
    a = np.random.permutation(np.resize(levels, k // 512 * 4)).reshape(k // 512, 4)
    idx = np.arange(k)
    return np.exp2(a[idx // 512, idx % 128 // 32])


BF16 = ml_dtypes.bfloat16


def bf(x):
    return np.asarray(x, np.float32).astype(BF16)


def f64(x):
    return np.asarray(x).astype(np.float64)


B, C, O, M, K, NR, NT = 2, 512, 256, 4, 32, 8, 8
BN_EPS = 1e-5


def setup_inputs():
    s = mx_kscale(C)

    def p(gain):
        return bf(np.random.standard_normal((O, C)) * gain / np.sqrt(C) / s[None, :])

    return {"A": bf(np.random.standard_normal((B, C, M, K, NR, NT)) * s[None, :, None, None, None, None]),
            "P1": p(1.0), "P2": p(2.0 * np.sqrt(M)), "P3": p(2.0 * np.sqrt(NT)), "P4": p(np.sqrt(NR)),
            "a5": bf(np.random.standard_normal((B, O, M, K, NT)) * 1.2 / np.sqrt(K)),
            "gamma": bf(1.0 + 0.2 * np.random.standard_normal(O)),
            "beta": bf(0.3 * np.random.standard_normal(O))}


def mix(P, X):
    y = mxq(f64(P), 1, "e4m3") @ mxq(X.reshape(B, C, -1), 1, "e4m3")
    return y.reshape((B, O) + X.shape[2:])


def reference(A, P1, P2, P3, P4, a5, gamma, beta):
    Af = f64(A)
    A1 = mix(P1, Af)
    A2 = mix(P2, Af.mean(2))[:, :, None]
    A3 = mix(P3, Af.mean(5))[..., None]
    A4 = mix(P4, Af.mean(4))[:, :, :, :, None, :]
    A5 = f64(a5)[:, :, :, :, None, :]
    y = A1 + 0.1 * A2 + 0.1 * A3 + 0.5 * A4 + 2.0 * A5
    y = np.maximum(y, 0.0)
    ax = (0, 2, 3, 4, 5)
    mean = y.mean(axis=ax, keepdims=True)
    var = y.var(axis=ax, keepdims=True)
    g = f64(gamma)[None, :, None, None, None, None]
    bta = f64(beta)[None, :, None, None, None, None]
    return (y - mean) * (1.0 / np.sqrt(var + BN_EPS)) * g + bta

@@ -1,0 +1,524 @@
+from contextlib import ExitStack
+
+import concourse.mybir as mybir
+from concourse.masks import make_identity
+
+BF16 = mybir.dt.bfloat16
+F32 = mybir.dt.float32
+I32 = mybir.dt.int32
+U32 = mybir.dt.uint32
+U8 = mybir.dt.uint8
+FP8X4 = mybir.dt.float8_e4m3fn_x4
+ALU = mybir.AluOpType
+ACT = mybir.ActivationFunctionType
+AXIS_X = mybir.AxisListType.X
+
+B, C, O, M, K, NR, NT = 2, 512, 256, 4, 32, 8, 8
+BN_EPS = 1e-5
+P = 128
+PACK = 4
+O_TILES = O // P
+POSITIONS = M * K * NR * NT
+
+K_PIECE = 4
+PIECES_PER_B = K // K_PIECE
+N_PIECES = B * PIECES_PER_B
+KR = K_PIECE * NR
+RUN = K_PIECE * NR * NT
+COLS = M * RUN
+SMALL = M * KR
+HALVES = RUN // P
+K_SQUARE = K_PIECE // HALVES
+T_RUN = NT // 2
+POOLED = K_SQUARE * NR
+SMALL_COLS = 2 * SMALL + RUN
+
+UP = 10.0
+STATIONARY = (("p1", 8.0), ("p1", 2.0), ("p2", 1.0 / M), ("p3", 1.0), ("p4", 1.0))
+W_A1_HI, W_A1_LO, W_A2, W_A3, W_A4 = 0, 1, 2, 3, 4
+
+FLOPS = 2 * O * C * B * POSITIONS * (8 + 2 + 1 + 1) // 8
+
+
+def tile_layer_3d_dep_pa_t_kernel(tc, A, P1, P2, P3, P4, a5, gamma, beta, out):
+    nc = tc.nc
+    weights = {"p1": P1, "p2": P2, "p3": P3, "p4": P4}
+
+    with ExitStack() as ctx:
+        keep = ctx.enter_context(tc.tile_pool(name="keep", bufs=1))
+        psum_x = ctx.enter_context(tc.psum_pool(name="psum_x", bufs=3))
+        psum_turned = ctx.enter_context(tc.psum_pool(name="psum_turned", bufs=2))
+        psum_pooled = ctx.enter_context(tc.psum_pool(name="psum_pooled", bufs=2))
+        psum_small = ctx.enter_context(tc.psum_pool(name="psum_small", bufs=1))
+
+        w_codes = keep.tile([P, len(STATIONARY), O], U32, align_bytes=64)
+        w_scales = keep.tile([P, len(STATIONARY), O], U8, align_bytes=64)
+        a5_sb = keep.tile([P, B * O_TILES, M * K * NT], BF16)
+        gamma_beta = keep.tile([P, 2 * O_TILES], F32)
+        y = keep.tile([P, O_TILES, N_PIECES, COLS], F32)
+        sums = keep.tile([P, O_TILES, N_PIECES], F32)
+        squares = keep.tile([P, O_TILES, N_PIECES], F32)
+        small_scales = [
+            keep.tile([P, SMALL_COLS], U8, align_bytes=64, name="small_scales%d" % parity)
+            for parity in range(2)
+        ]
+        for parity in range(2):
+            nc.vector.memset(small_scales[parity][:].bitcast(I32), 0)
+        ident_bf16 = keep.tile([P, P], BF16)
+        make_identity(nc, ident_bf16[:])
+        pool_mat = keep.tile([P, 2, POOLED], BF16)
+
+        table_warmer = keep.tile([P, 1], F32)
+        nc.vector.memset(table_warmer[:], 1.0)
+        nc.scalar.sqrt(out=table_warmer[:], in_=table_warmer[:])
+
+        raw_pool = ctx.enter_context(tc.tile_pool(name="raw_pool", bufs=3))
+
+        def load(piece):
+            b, kq = divmod(piece, PIECES_PER_B)
+            raw = raw_pool.tile([P, PACK, M, RUN], BF16, name="raw")
+            nc.sync.dma_start(
+                out=raw[:],
+                in_=A[b].rearrange("(p j) m k r t -> p j m (k r t)", j=PACK)[
+                    :, :, :, kq * RUN : (kq + 1) * RUN
+                ],
+            )
+            return raw
+
+        ctx.enter_context(tc.manual_schedule())
+
+        with tc.tile_pool(name="setup", bufs=2) as setup:
+            gb_rows = setup.tile([P, P], BF16, tag="gb_rows")
+            nc.vector.memset(gb_rows[:], 0.0)
+            ident_f32 = setup.tile([P, P], F32, tag="ident_f32")
+            make_identity(nc, ident_f32[:])
+
+            pool_ones = setup.tile([P, 2, POOLED], F32, tag="pool_ones")
+            nc.vector.tensor_reduce(
+                out=pool_ones[:, 0, :],
+                in_=ident_f32[:].rearrange("p (x t) -> p x t", t=NT),
+                axis=AXIS_X,
+                op=ALU.add,
+            )
+            nc.vector.tensor_reduce(
+                out=pool_ones[:, 1, :].rearrange("p (k t) -> p k t", t=NT),
+                in_=ident_f32[:].rearrange("p (k r t) -> p k t r", r=NR, t=NT),
+                axis=AXIS_X,
+                op=ALU.add,
+            )
+            nc.vector.tensor_scalar_mul(out=pool_mat[:, 0, :], in0=pool_ones[:, 0, :], scalar1=1.0 / NT)
+            nc.vector.tensor_scalar_mul(out=pool_mat[:, 1, :], in0=pool_ones[:, 1, :], scalar1=1.0 / NR)
+
+            all_w_rows = {}
+            for name in ("p1", "p2", "p3", "p4"):
+                w_rows = setup.tile([P, O_TILES, C], BF16, name="w_rows_" + name, bufs=1)
+                nc.sync.dma_start(
+                    out=w_rows[:], in_=weights[name].rearrange("(ot o) c -> o ot c", o=P)
+                )
+                all_w_rows[name] = w_rows
+            nc.sync.dma_start(out=gb_rows[0:O_TILES, :], in_=gamma.rearrange("(ot o) -> ot o", o=P))
+            nc.sync.dma_start(
+                out=gb_rows[O_TILES : 2 * O_TILES, :], in_=beta.rearrange("(ot o) -> ot o", o=P)
+            )
+            first_raws = {0: load(0), 1: load(1)}
+            nc.sync.dma_start(
+                out=a5_sb[:], in_=a5.rearrange("b (ot o) m k t -> o (b ot) (m k t)", o=P)
+            )
+            first_raws[2] = load(2)
+
+            grouped_w = {}
+            for name in ("p1", "p2", "p3", "p4"):
+                w_rows = all_w_rows[name]
+                words = w_rows[:].bitcast(F32).rearrange("o ot (p u) -> o ot u p", u=2)
+                turned = psum_x.tile([P, O_TILES, 2, P], F32, name="acc")
+                for ot in range(O_TILES):
+                    for u in range(2):
+                        nc.tensor.transpose(turned[:, ot, u, :], words[:, ot, u, :], ident_f32[:])
+                grouped = setup.tile([P, O * PACK], BF16, name="grouped_" + name, bufs=1, align_bytes=64)
+                nc.scalar.copy(
+                    out=grouped[:].bitcast(F32).rearrange("p (ot o u) -> p ot o u", ot=O_TILES, u=2),
+                    in_=turned[:].rearrange("p ot u o -> p ot o u"),
+                )
+                grouped_w[name] = grouped
+
+            for i, (name, factor) in enumerate(STATIONARY):
+                scaled = grouped_w[name]
+                if factor != 1.0:
+                    scaled = setup.tile([P, O * PACK], BF16, tag="scaled", align_bytes=64)
+                    nc.vector.tensor_scalar_mul(out=scaled[:], in0=grouped_w[name][:], scalar1=factor)
+                nc.vector.quantize_mx(
+                    out=w_codes[:, i, :].bitcast(FP8X4), scales=w_scales[:, i, :], in_=scaled[:]
+                )
+
+            gb_turned = psum_small.tile([P, P], BF16, tag="small")
+            nc.tensor.transpose(gb_turned[:], gb_rows[:], ident_bf16[:])
+            nc.vector.tensor_copy(out=gamma_beta[:], in_=gb_turned[:, 0 : 2 * O_TILES])
+
+        with tc.tile_pool(name="once", bufs=1) as once, tc.tile_pool(name="twice", bufs=2) as twice:
+
+            def mix(acc, weight, ot, codes, scales, start, stop):
+                nc.tensor.matmul_mx(
+                    out=acc,
+                    lhsT=w_codes[:, weight, ot * P : (ot + 1) * P].bitcast(FP8X4),
+                    lhsT_scale=w_scales[:, weight, ot * P : (ot + 1) * P],
+                    rhs=codes.bitcast(FP8X4),
+                    rhs_scale=scales,
+                    start=start,
+                    stop=stop,
+                )
+
+            tiles = {("raw", piece): first_raws[piece] for piece in first_raws}
+
+            def regroup_a_scalar(piece):
+                raw = tiles["raw", piece]
+                grouped_a = once.tile([P, COLS, PACK], BF16, align_bytes=64, name="grouped_a")
+                target = grouped_a[:].rearrange("p (m th tl x) j -> p th m x j tl", m=M, tl=T_RUN, x=KR)
+                source = raw[:].rearrange("p j m (x th tl) -> p th m x j tl", x=KR, tl=T_RUN)
+                for m in range(M // 2, M):
+                    nc.scalar.copy(out=target[:, 1, m], in_=source[:, 1, m])
+                tiles["grouped_a", piece] = grouped_a
+                tiles["regroup_views", piece] = (target, source)
+
+            def regroup_a_vector(piece):
+                target, source = tiles["regroup_views", piece]
+                nc.vector.tensor_copy(out=target[:, 0], in_=source[:, 0])
+                nc.vector.tensor_copy(out=target[:, 1, 0 : M // 2], in_=source[:, 1, 0 : M // 2])
+
+            def sum_pairs_of_m(piece):
+                by_m = tiles["grouped_a", piece][:].rearrange("p (m w) j -> p m (w j)", m=M)
+                pair_sums = once.tile([P, 2, RUN * PACK], F32, name="pair_sums")
+                nc.vector.tensor_add(out=pair_sums[:], in0=by_m[:, 0:2, :], in1=by_m[:, 2:4, :])
+                tiles["pair_sums", piece] = pair_sums
+
+            def quantise_a(piece):
+                a_codes = twice.tile([P, COLS], U32, align_bytes=64, name="a_codes")
+                a_scales = twice.tile([P, COLS], U8, align_bytes=64, name="a_scales")
+                nc.vector.quantize_mx(
+                    out=a_codes[:].bitcast(FP8X4),
+                    scales=a_scales[:],
+                    in_=tiles["grouped_a", piece][:].rearrange("p w j -> p (w j)"),
+                )
+                tiles["a_codes", piece], tiles["a_scales", piece] = a_codes, a_scales
+
+            def finish_sum_over_m(piece):
+                pair_sums = tiles["pair_sums", piece]
+                grouped_small = once.tile([P, SMALL_COLS * PACK], BF16, align_bytes=64, name="grouped_small")
+                nc.vector.tensor_add(
+                    out=grouped_small[:, 2 * SMALL * PACK :], in0=pair_sums[:, 0, :], in1=pair_sums[:, 1, :]
+                )
+                tiles["grouped_small", piece] = grouped_small
+
+            def turn(piece, j):
+                raw = tiles["raw", piece]
+                turned_ps = psum_turned.tile([P, M, HALVES, P], BF16, name="turned_ps")
+                for m in range(M):
+                    for h in range(HALVES):
+                        nc.tensor.transpose(
+                            turned_ps[:, m, h, :], raw[:, j, m, h * P : (h + 1) * P], ident_bf16[:]
+                        )
+                turned = twice.tile([P, M, HALVES, P], BF16, name="turned")
+                nc.scalar.copy(
+                    out=turned[:].rearrange("p m h c -> p (m h c)").bitcast(F32),
+                    in_=turned_ps[:].rearrange("p m h c -> p (m h c)").bitcast(F32),
+                )
+                tiles["turned", piece, j] = turned
+
+            def pool(piece, j):
+                if j == 0:
+                    for i in range(M // 2):
+                        tiles["pooled", piece, i] = psum_pooled.tile(
+                            [P, 2, PACK, 2, HALVES, POOLED], F32, name="pooled%d" % i, tag="pooled"
+                        )
+                for m in range(M):
+                    for h in range(HALVES):
+                        nc.tensor.matmul(
+                            out=tiles["pooled", piece, m // 2][:, :, j, m % 2, h, :],
+                            lhsT=tiles["turned", piece, j][:, m, h, :],
+                            rhs=pool_mat[:],
+                            start=True,
+                            stop=True,
+                        )
+
+            def round_means(piece):
+                grouped_tr = tiles["grouped_small", piece][:, 0 : 2 * SMALL * PACK].rearrange(
+                    "p (s w j) -> p s w j", s=2, j=PACK
+                )
+                for i in range(M // 2):
+                    nc.scalar.copy(
+                        out=grouped_tr[:, :, i * (SMALL // 2) : (i + 1) * (SMALL // 2), :],
+                        in_=tiles["pooled", piece, i][:].rearrange("p s j m h x -> p s (m h x) j"),
+                    )
+
+            def quantise_means(piece):
+                small_codes = twice.tile([P, SMALL_COLS], U32, align_bytes=64, name="small_codes")
+                scales = small_scales[piece % 2]
+                nc.vector.quantize_mx(
+                    out=small_codes[:, 0 : 2 * SMALL].bitcast(FP8X4),
+                    scales=scales[:, 0 : 2 * SMALL],
+                    in_=tiles["grouped_small", piece][:, 0 : 2 * SMALL * PACK],
+                )
+                at_rep_codes = twice.tile([P, COLS], U32, align_bytes=64, name="at_rep_codes")
+                at_rep_scales = twice.tile([P, COLS], U8, align_bytes=64, name="at_rep_scales")
+                for m in range(M):
+                    nc.sync.dma_start(
+                        out=at_rep_codes[:, m * RUN : (m + 1) * RUN]
+                        .bitcast(I32)
+                        .rearrange("p (t x) -> p t x", t=NT),
+                        in_=small_codes[:, m * KR : (m + 1) * KR]
+                        .bitcast(I32)
+                        .unsqueeze(1)
+                        .to_broadcast([P, NT, KR]),
+                    )
+                tiles["small_codes", piece] = small_codes
+                tiles["at_rep_codes", piece], tiles["at_rep_scales", piece] = at_rep_codes, at_rep_scales
+
+            def repeat_scales(piece):
+                nc.vector.tensor_copy(
+                    out=tiles["at_rep_scales", piece][:]
+                    .bitcast(I32)
+                    .rearrange("p (m t x) -> p m t x", m=M, t=NT),
+                    in_=small_scales[piece % 2][:, 0:SMALL]
+                    .bitcast(I32)
+                    .rearrange("p (m x) -> p m x", m=M)
+                    .unsqueeze(2)
+                    .to_broadcast([P, M, NT, KR // 4]),
+                )
+
+            def quantise_sum_over_m(piece):
+                nc.vector.quantize_mx(
+                    out=tiles["small_codes", piece][:, 2 * SMALL :].bitcast(FP8X4),
+                    scales=small_scales[piece % 2][:, 2 * SMALL :],
+                    in_=tiles["grouped_small", piece][:, 2 * SMALL * PACK :],
+                )
+
+            def scale_a5(piece):
+                b, kq = divmod(piece, PIECES_PER_B)
+                a5_of_b = a5_sb[:].rearrange("p g x -> p (g x)")[
+                    :, b * O_TILES * M * K * NT : (b + 1) * O_TILES * M * K * NT
+                ]
+                a5_scaled = twice.tile([P, O_TILES * M, NT * K_PIECE], F32, name="a5_scaled")
+                nc.gpsimd.tensor_scalar(
+                    out=a5_scaled[:].rearrange("p g (t k) -> p g t k", t=NT),
+                    in0=a5_of_b.rearrange(
+                        "p (g kq k t) -> p kq g t k", kq=PIECES_PER_B, k=K_PIECE, t=NT
+                    )[:, kq],
+                    scalar1=2.0 / 0.5,
+                    scalar2=0.0,
+                    op0=ALU.mult,
+                    op1=ALU.add,
+                )
+                tiles["a5_scaled", piece] = a5_scaled
+
+            def terms_without_r(piece):
+                ar_codes = tiles["small_codes", piece][:, SMALL : 2 * SMALL]
+                ar_scales = small_scales[piece % 2][:, SMALL : 2 * SMALL]
+                a4_acc = psum_small.tile([P, O_TILES * SMALL], F32, tag="small", name="a4_acc")
+                for ot in range(O_TILES):
+                    a4_cols = a4_acc[:, ot * SMALL : (ot + 1) * SMALL]
+                    mix(a4_cols, W_A4, ot, ar_codes, ar_scales, True, True)
+                no_r = twice.tile([P, O_TILES * M, NT * K_PIECE], F32, name="no_r")
+                nc.vector.tensor_tensor(
+                    out=no_r[:].rearrange("p g (t k) -> p g t k", t=NT),
+                    in0=a4_acc[:].rearrange("p (g k t) -> p g t k", k=K_PIECE, t=NT),
+                    in1=tiles["a5_scaled", piece][:].rearrange("p g (t k) -> p g t k", t=NT),
+                    op=ALU.add,
+                )
+                tiles["no_r", piece] = no_r
+
+            def mix_bank(piece, bank):
+                ot, m_pair = divmod(bank, M // 2)
+                acc = psum_x.tile([P, 2, RUN], F32, name="acc")
+                am_codes = tiles["small_codes", piece][:, 2 * SMALL :]
+                am_scales = small_scales[piece % 2][:, 2 * SMALL :]
+                for i in range(2):
+                    cols = slice((2 * m_pair + i) * RUN, (2 * m_pair + i + 1) * RUN)
+                    a_codes, a_scales = tiles["a_codes", piece][:, cols], tiles["a_scales", piece][:, cols]
+                    mix(acc[:, i, :], W_A1_HI, ot, a_codes, a_scales, True, False)
+                    mix(acc[:, i, :], W_A1_LO, ot, a_codes, a_scales, False, False)
+                    mix(acc[:, i, :], W_A2, ot, am_codes, am_scales, False, False)
+                    mix(
+                        acc[:, i, :], W_A3, ot, tiles["at_rep_codes", piece][:, cols],
+                        tiles["at_rep_scales", piece][:, cols], False, True,
+                    )
+                tiles["acc", piece, bank] = acc
+
+            def add_out(piece, bank):
+                ot, m_pair = divmod(bank, M // 2)
+                acc = tiles["acc", piece, bank]
+                g = ot * M + 2 * m_pair
+                nc.vector.scalar_tensor_tensor(
+                    out=y[:, ot, piece, 2 * m_pair * RUN : (2 * m_pair + 2) * RUN].rearrange(
+                        "p (x r) -> p x r", r=NR
+                    ),
+                    in0=tiles["no_r", piece][:, g : g + 2, :]
+                    .rearrange("p g x -> p (g x)")
+                    .unsqueeze(2)
+                    .to_broadcast([P, 2 * NT * K_PIECE, NR]),
+                    scalar=0.5 * UP,
+                    in1=acc[:].rearrange("p i (x r) -> p (i x) r", r=NR),
+                    op0=ALU.mult,
+                    op1=ALU.add,
+                )
+
+            def activate(piece, part):
+                ot, second = divmod(part, 2)
+                y_piece = y[:, ot, piece, :]
+                if not second:
+                    nc.scalar.activation(
+                        out=y_piece, in_=y_piece, func=ACT.Relu,
+                        accum_out=sums[:, ot, piece : piece + 1],
+                    )
+                else:
+                    squared = twice.tile([P, COLS], BF16, name="squared")
+                    nc.scalar.activation(
+                        out=squared[:], in_=y_piece, func=ACT.Square,
+                        accum_out=squares[:, ot, piece : piece + 1],
+                    )
+
+            assert PACK == O_TILES * (M // 2)
+            LAST = PACK - 1
+            turn(0, 0)
+            turn(0, 1)
+            pool(0, 0)
+            for i in range(-1, N_PIECES):
+                ahead, here, behind = i + 1, i, i - 1
+                prepares = ahead < N_PIECES
+                turns_next = ahead + 1 < N_PIECES
+                multiplies = 0 <= here < N_PIECES
+                finishes = 0 <= behind < N_PIECES
+                if 3 <= ahead + 2 < N_PIECES:
+                    tiles["raw", ahead + 2] = load(ahead + 2)
+                if finishes:
+                    add_out(behind, LAST)
+                if prepares:
+                    scale_a5(ahead)
+                    regroup_a_scalar(ahead)
+                if prepares:
+                    turn(ahead, 2)
+                    pool(ahead, 1)
+                if multiplies:
+                    terms_without_r(here)
+                if prepares:
+                    regroup_a_vector(ahead)
+                if multiplies:
+                    mix_bank(here, 0)
+                    add_out(here, 0)
+                if finishes:
+                    activate(behind, 0)
+                if prepares:
+                    turn(ahead, 3)
+                    pool(ahead, 2)
+                    sum_pairs_of_m(ahead)
+                if multiplies:
+                    mix_bank(here, 1)
+                    add_out(here, 1)
+                if finishes:
+                    activate(behind, 1)
+                    activate(behind, 2)
+                if prepares:
+                    pool(ahead, 3)
+                    finish_sum_over_m(ahead)
+                    round_means(ahead)
+                if turns_next:
+                    turn(ahead + 1, 0)
+                if prepares:
+                    quantise_means(ahead)
+                    quantise_a(ahead)
+                    quantise_sum_over_m(ahead)
+                    repeat_scales(ahead)
+                if multiplies:
+                    mix_bank(here, 2)
+                    add_out(here, 2)
+                if finishes:
+                    activate(behind, 3)
+                if turns_next:
+                    turn(ahead + 1, 1)
+                    pool(ahead + 1, 0)
+                if multiplies:
+                    mix_bank(here, LAST)
+
+            count = float(B * POSITIONS)
+            total = keep.tile([P, O_TILES], F32)
+            total_sq = keep.tile([P, O_TILES], F32)
+            mean_sq = keep.tile([P, O_TILES], F32)
+            var = keep.tile([P, O_TILES], F32)
+            std = keep.tile([P, O_TILES], F32)
+            gain = keep.tile([P, O_TILES], F32)
+            shift = keep.tile([P, O_TILES], F32)
+
+            def variance(ot):
+                col = slice(ot, ot + 1)
+                nc.vector.tensor_reduce(out=total[:, col], in_=sums[:, ot, :], axis=AXIS_X, op=ALU.add)
+                nc.vector.tensor_reduce(out=total_sq[:, col], in_=squares[:, ot, :], axis=AXIS_X, op=ALU.add)
+                nc.vector.scalar_tensor_tensor(
+                    out=mean_sq[:, col], in0=total[:, col], scalar=1.0 / (count * count), in1=total[:, col],
+                    op0=ALU.mult, op1=ALU.mult,
+                )
+                nc.vector.scalar_tensor_tensor(
+                    out=var[:, col], in0=total_sq[:, col], scalar=1.0 / count, in1=mean_sq[:, col],
+                    op0=ALU.mult, op1=ALU.subtract,
+                )
+                nc.vector.tensor_scalar(
+                    out=var[:, col], in0=var[:, col], scalar1=0.0, scalar2=BN_EPS * UP * UP,
+                    op0=ALU.max, op1=ALU.add,
+                )
+
+            def gain_and_shift(ot):
+                col = slice(ot, ot + 1)
+                nc.vector.reciprocal(out=gain[:, col], in_=std[:, col])
+                nc.vector.tensor_mul(out=gain[:, col], in0=gain[:, col], in1=gamma_beta[:, col])
+                nc.vector.scalar_tensor_tensor(
+                    out=shift[:, col], in0=total[:, col], scalar=1.0 / count, in1=gain[:, col],
+                    op0=ALU.mult, op1=ALU.mult,
+                )
+                nc.vector.tensor_sub(
+                    out=shift[:, col], in0=gamma_beta[:, O_TILES + ot : O_TILES + ot + 1], in1=shift[:, col]
+                )
+
+            def normalise(ot, step, staged):
+                b, m = divmod(step, M)
+                source = y[
+                    :, ot, b * PIECES_PER_B : (b + 1) * PIECES_PER_B, m * RUN : (m + 1) * RUN
+                ].rearrange("p q (th tl x) -> p th q x tl", tl=T_RUN, x=KR)
+                target = staged[:].rearrange("p q x (th tl) -> p th q x tl", tl=T_RUN)
+                for th in range(NT // T_RUN):
+                    if step % 2 == 0:
+                        nc.vector.tensor_scalar(
+                            out=target[:, th], in0=source[:, th], scalar1=gain[:, ot : ot + 1],
+                            scalar2=shift[:, ot : ot + 1], op0=ALU.mult, op1=ALU.add,
+                        )
+                    else:
+                        nc.scalar.activation(
+                            out=target[:, th], in_=source[:, th], func=ACT.Identity,
+                            bias=shift[:, ot : ot + 1], scale=gain[:, ot : ot + 1],
+                        )
+                nc.sync.dma_start(
+                    out=out[b].rearrange("(ot o) m k r t -> o ot m (k r t)", o=P)[:, ot, m, :],
+                    in_=staged[:].rearrange("p q x t -> p (q x t)"),
+                )
+
+            def stage_in_raw_buffer():
+                return raw_pool.tile([P, PIECES_PER_B, KR, NT], F32, name="raw")
+
+            final = N_PIECES - 1
+            activate(final, 0)
+            activate(final, 1)
+            variance(0)
+            nc.scalar.sqrt(out=std[:, 0:1], in_=var[:, 0:1])
+            add_out(final, LAST)
+            activate(final, 2)
+            activate(final, 3)
+            gain_and_shift(0)
+            normalise(0, 0, stage_in_raw_buffer())
+            variance(1)
+            normalise(0, 1, stage_in_raw_buffer())
+            nc.scalar.sqrt(out=std[:, 1:2], in_=var[:, 1:2])
+            normalise(0, 2, stage_in_raw_buffer())
+            gain_and_shift(1)
+            for step in range(3, B * M):
+                normalise(0, step, stage_in_raw_buffer())
+
+        staged_pool = ctx.enter_context(tc.tile_pool(name="staged_pool", bufs=4))
+        for step in range(B * M):
+            staged = staged_pool.tile([P, PIECES_PER_B, KR, NT], F32)
+            normalise(1, step, staged)

@@ -56,8 +56,8 @@ def tile_layer_3d_dep_pa_t_kernel(tc, A, P1, P2, P3, P4, a5, gamma, beta, out):
         a5_sb = keep.tile([P, B * O_TILES, M * K * NT], BF16)
         gamma_beta = keep.tile([P, 2 * O_TILES], F32)
         y = keep.tile([P, O_TILES, N_PIECES, COLS], F32)
-        sums = keep.tile([P, O_TILES, N_PIECES], F32)
-        squares = keep.tile([P, O_TILES, N_PIECES], F32)
+        sums = keep.tile([P, O_TILES, N_PIECES + 1], F32)
+        squares = keep.tile([P, O_TILES, N_PIECES + 1], F32)
         small_scales = [
             keep.tile([P, SMALL_COLS], U8, align_bytes=64, name="small_scales%d" % parity)
             for parity in range(2)
@@ -87,69 +87,82 @@ def tile_layer_3d_dep_pa_t_kernel(tc, A, P1, P2, P3, P4, a5, gamma, beta, out):
 
         ctx.enter_context(tc.manual_schedule())
 
-        with tc.tile_pool(name="setup", bufs=2) as setup:
-            gb_rows = setup.tile([P, P], BF16, tag="gb_rows")
-            nc.vector.memset(gb_rows[:], 0.0)
-            ident_f32 = setup.tile([P, P], F32, tag="ident_f32")
-            make_identity(nc, ident_f32[:])
+        setup = ctx.enter_context(tc.tile_pool(name="setup", bufs=1))
+        gb_rows = setup.tile([P, P], BF16, name="gb_rows")
+        nc.vector.memset(gb_rows[:], 0.0)
+        ident_f32 = setup.tile([P, P], F32, name="ident_f32")
+        make_identity(nc, ident_f32[:])
 
-            pool_ones = setup.tile([P, 2, POOLED], F32, tag="pool_ones")
-            nc.vector.tensor_reduce(
-                out=pool_ones[:, 0, :],
-                in_=ident_f32[:].rearrange("p (x t) -> p x t", t=NT),
-                axis=AXIS_X,
-                op=ALU.add,
-            )
-            nc.vector.tensor_reduce(
-                out=pool_ones[:, 1, :].rearrange("p (k t) -> p k t", t=NT),
-                in_=ident_f32[:].rearrange("p (k r t) -> p k t r", r=NR, t=NT),
-                axis=AXIS_X,
-                op=ALU.add,
-            )
-            nc.vector.tensor_scalar_mul(out=pool_mat[:, 0, :], in0=pool_ones[:, 0, :], scalar1=1.0 / NT)
-            nc.vector.tensor_scalar_mul(out=pool_mat[:, 1, :], in0=pool_ones[:, 1, :], scalar1=1.0 / NR)
+        w_rows = raw_pool.tile([P, len(weights), O_TILES, C], BF16, name="raw")
 
-            all_w_rows = {}
-            for name in ("p1", "p2", "p3", "p4"):
-                w_rows = setup.tile([P, O_TILES, C], BF16, name="w_rows_" + name, bufs=1)
-                nc.sync.dma_start(
-                    out=w_rows[:], in_=weights[name].rearrange("(ot o) c -> o ot c", o=P)
-                )
-                all_w_rows[name] = w_rows
-            nc.sync.dma_start(out=gb_rows[0:O_TILES, :], in_=gamma.rearrange("(ot o) -> ot o", o=P))
+        def load_weight(n, name):
             nc.sync.dma_start(
-                out=gb_rows[O_TILES : 2 * O_TILES, :], in_=beta.rearrange("(ot o) -> ot o", o=P)
+                out=w_rows[:, n], in_=weights[name].rearrange("(ot o) c -> o ot c", o=P)
             )
-            first_raws = {0: load(0), 1: load(1)}
-            nc.sync.dma_start(
-                out=a5_sb[:], in_=a5.rearrange("b (ot o) m k t -> o (b ot) (m k t)", o=P)
+
+        load_weight(0, "p1")
+        first_raws = {0: load(0)}
+        for n, name in enumerate(("p2", "p3", "p4")):
+            load_weight(n + 1, name)
+        first_raws[1] = load(1)
+        nc.sync.dma_start(out=gb_rows[0:O_TILES, :], in_=gamma.rearrange("(ot o) -> ot o", o=P))
+        nc.sync.dma_start(
+            out=gb_rows[O_TILES : 2 * O_TILES, :], in_=beta.rearrange("(ot o) -> ot o", o=P)
+        )
+        nc.sync.dma_start(
+            out=a5_sb[:], in_=a5.rearrange("b (ot o) m k t -> o (b ot) (m k t)", o=P)
+        )
+
+        pool_ones = setup.tile([P, 2, POOLED], F32, name="pool_ones")
+        nc.vector.tensor_reduce(
+            out=pool_ones[:, 0, :],
+            in_=ident_f32[:].rearrange("p (x t) -> p x t", t=NT),
+            axis=AXIS_X,
+            op=ALU.add,
+        )
+        nc.vector.tensor_reduce(
+            out=pool_ones[:, 1, :].rearrange("p (k t) -> p k t", t=NT),
+            in_=ident_f32[:].rearrange("p (k r t) -> p k t r", r=NR, t=NT),
+            axis=AXIS_X,
+            op=ALU.add,
+        )
+        nc.vector.tensor_scalar_mul(out=pool_mat[:, 0, :], in0=pool_ones[:, 0, :], scalar1=1.0 / NT)
+        nc.vector.tensor_scalar_mul(out=pool_mat[:, 1, :], in0=pool_ones[:, 1, :], scalar1=1.0 / NR)
+
+        grouped_w = {}
+
+        def group_weight(n, name):
+            words = w_rows[:, n].bitcast(F32).rearrange("o ot (p u) -> o ot u p", u=2)
+            turned = psum_x.tile([P, O_TILES, 2, P], F32, name="acc")
+            for ot in range(O_TILES):
+                for u in range(2):
+                    nc.tensor.transpose(turned[:, ot, u, :], words[:, ot, u, :], ident_f32[:])
+            grouped = setup.tile([P, O * PACK], BF16, name="grouped_" + name, align_bytes=64)
+            nc.scalar.copy(
+                out=grouped[:].bitcast(F32).rearrange("p (ot o u) -> p ot o u", ot=O_TILES, u=2),
+                in_=turned[:].rearrange("p ot u o -> p ot o u"),
             )
-            first_raws[2] = load(2)
+            grouped_w[name] = grouped
 
-            grouped_w = {}
-            for name in ("p1", "p2", "p3", "p4"):
-                w_rows = all_w_rows[name]
-                words = w_rows[:].bitcast(F32).rearrange("o ot (p u) -> o ot u p", u=2)
-                turned = psum_x.tile([P, O_TILES, 2, P], F32, name="acc")
-                for ot in range(O_TILES):
-                    for u in range(2):
-                        nc.tensor.transpose(turned[:, ot, u, :], words[:, ot, u, :], ident_f32[:])
-                grouped = setup.tile([P, O * PACK], BF16, name="grouped_" + name, bufs=1, align_bytes=64)
-                nc.scalar.copy(
-                    out=grouped[:].bitcast(F32).rearrange("p (ot o u) -> p ot o u", ot=O_TILES, u=2),
-                    in_=turned[:].rearrange("p ot u o -> p ot o u"),
-                )
-                grouped_w[name] = grouped
+        def quantise_weight(i):
+            name, factor = STATIONARY[i]
+            scaled = grouped_w[name]
+            if factor != 1.0:
+                scaled = setup.tile([P, O * PACK], BF16, name="scaled%d" % (i % 2), align_bytes=64)
+                nc.vector.tensor_scalar_mul(out=scaled[:], in0=grouped_w[name][:], scalar1=factor)
+            nc.vector.quantize_mx(
+                out=w_codes[:, i, :].bitcast(FP8X4), scales=w_scales[:, i, :], in_=scaled[:]
+            )
 
-            for i, (name, factor) in enumerate(STATIONARY):
-                scaled = grouped_w[name]
-                if factor != 1.0:
-                    scaled = setup.tile([P, O * PACK], BF16, tag="scaled", align_bytes=64)
-                    nc.vector.tensor_scalar_mul(out=scaled[:], in0=grouped_w[name][:], scalar1=factor)
-                nc.vector.quantize_mx(
-                    out=w_codes[:, i, :].bitcast(FP8X4), scales=w_scales[:, i, :], in_=scaled[:]
-                )
+        group_weight(0, "p1")
+        for i in (W_A1_HI, W_A1_LO):
+            quantise_weight(i)
 
+        def finish_weights():
+            for i in (W_A2, W_A3, W_A4):
+                quantise_weight(i)
+
+        def turn_gamma_beta():
             gb_turned = psum_small.tile([P, P], BF16, tag="small")
             nc.tensor.transpose(gb_turned[:], gb_rows[:], ident_bf16[:])
             nc.vector.tensor_copy(out=gamma_beta[:], in_=gb_turned[:, 0 : 2 * O_TILES])
@@ -375,10 +388,40 @@ def tile_layer_3d_dep_pa_t_kernel(tc, A, P1, P2, P3, P4, a5, gamma, beta, out):
                         accum_out=squares[:, ot, piece : piece + 1],
                     )
 
+            final = N_PIECES - 1
+
+            def last_bank(bank):
+                ot, half = divmod(bank, M // 2)
+                col = final + half
+                part = y[:, ot, final, half * 2 * RUN : (half + 1) * 2 * RUN]
+                return part, sums[:, ot, col : col + 1], squares[:, ot, col : col + 1]
+
+            def last_relu_scalar(bank):
+                part, sum_col, square_col = last_bank(bank)
+                nc.scalar.activation(out=part, in_=part, func=ACT.Relu, accum_out=sum_col)
+
+            def last_relu_vector(bank):
+                part, sum_col, square_col = last_bank(bank)
+                nc.vector.tensor_scalar(
+                    out=part, in0=part, scalar1=0.0, scalar2=0.0, op0=ALU.max, op1=ALU.add,
+                    accum_out=sum_col,
+                )
+
+            def last_square(bank):
+                part, sum_col, square_col = last_bank(bank)
+                squared = twice.tile([P, COLS], BF16, name="squared")
+                nc.scalar.activation(
+                    out=squared[:, 0 : 2 * RUN], in_=part, func=ACT.Square, accum_out=square_col
+                )
+
             assert PACK == O_TILES * (M // 2)
             LAST = PACK - 1
+            regroup_a_scalar(0)
             turn(0, 0)
             turn(0, 1)
+            for n, name in enumerate(("p2", "p3", "p4")):
+                group_weight(n + 1, name)
+            tiles["raw", 2] = load(2)
             pool(0, 0)
             for i in range(-1, N_PIECES):
                 ahead, here, behind = i + 1, i, i - 1
@@ -392,7 +435,8 @@ def tile_layer_3d_dep_pa_t_kernel(tc, A, P1, P2, P3, P4, a5, gamma, beta, out):
                     add_out(behind, LAST)
                 if prepares:
                     scale_a5(ahead)
-                    regroup_a_scalar(ahead)
+                    if ahead > 0:
+                        regroup_a_scalar(ahead)
                 if prepares:
                     turn(ahead, 2)
                     pool(ahead, 1)
@@ -409,12 +453,21 @@ def tile_layer_3d_dep_pa_t_kernel(tc, A, P1, P2, P3, P4, a5, gamma, beta, out):
                     turn(ahead, 3)
                     pool(ahead, 2)
                     sum_pairs_of_m(ahead)
+                    if ahead == 0:
+                        finish_weights()
+                    if ahead == 2:
+                        turn_gamma_beta()
                 if multiplies:
                     mix_bank(here, 1)
                     add_out(here, 1)
                 if finishes:
                     activate(behind, 1)
                     activate(behind, 2)
+                if here == final:
+                    last_relu_scalar(0)
+                    last_square(0)
+                    last_relu_vector(1)
+                    last_square(1)
                 if prepares:
                     pool(ahead, 3)
                     finish_sum_over_m(ahead)
@@ -429,7 +482,7 @@ def tile_layer_3d_dep_pa_t_kernel(tc, A, P1, P2, P3, P4, a5, gamma, beta, out):
                 if multiplies:
                     mix_bank(here, 2)
                     add_out(here, 2)
-                if finishes:
+                if finishes and here != final:
                     activate(behind, 3)
                 if turns_next:
                     turn(ahead + 1, 1)
@@ -500,22 +553,23 @@ def tile_layer_3d_dep_pa_t_kernel(tc, A, P1, P2, P3, P4, a5, gamma, beta, out):
             def stage_in_raw_buffer():
                 return raw_pool.tile([P, PIECES_PER_B, KR, NT], F32, name="raw")
 
-            final = N_PIECES - 1
-            activate(final, 0)
-            activate(final, 1)
             variance(0)
             nc.scalar.sqrt(out=std[:, 0:1], in_=var[:, 0:1])
             add_out(final, LAST)
-            activate(final, 2)
-            activate(final, 3)
             gain_and_shift(0)
             normalise(0, 0, stage_in_raw_buffer())
-            variance(1)
             normalise(0, 1, stage_in_raw_buffer())
-            nc.scalar.sqrt(out=std[:, 1:2], in_=var[:, 1:2])
+            activate(final - 1, 3)
+            for bank in (2, 3):
+                last_relu_vector(bank)
+                last_square(bank)
             normalise(0, 2, stage_in_raw_buffer())
+            variance(1)
+            normalise(0, 3, stage_in_raw_buffer())
+            nc.scalar.sqrt(out=std[:, 1:2], in_=var[:, 1:2])
+            normalise(0, 4, stage_in_raw_buffer())
             gain_and_shift(1)
-            for step in range(3, B * M):
+            for step in range(5, B * M):
                 normalise(0, step, stage_in_raw_buffer())
 
         staged_pool = ctx.enter_context(tc.tile_pool(name="staged_pool", bufs=4))

@@ -167,7 +167,9 @@ def tile_layer_3d_dep_pa_t_kernel(tc, A, P1, P2, P3, P4, a5, gamma, beta, out):
             nc.tensor.transpose(gb_turned[:], gb_rows[:], ident_bf16[:])
             nc.vector.tensor_copy(out=gamma_beta[:], in_=gb_turned[:, 0 : 2 * O_TILES])
 
-        with tc.tile_pool(name="once", bufs=1) as once, tc.tile_pool(name="twice", bufs=2) as twice:
+        with tc.tile_pool(name="once", bufs=1) as once, tc.tile_pool(name="twice", bufs=2) as twice, tc.tile_pool(
+            name="thrice", bufs=3
+        ) as thrice:
 
             def mix(acc, weight, ot, codes, scales, start, stop):
                 nc.tensor.matmul_mx(
@@ -215,11 +217,10 @@ def tile_layer_3d_dep_pa_t_kernel(tc, A, P1, P2, P3, P4, a5, gamma, beta, out):
 
             def finish_sum_over_m(piece):
                 pair_sums = tiles["pair_sums", piece]
-                grouped_small = once.tile([P, SMALL_COLS * PACK], BF16, align_bytes=64, name="grouped_small")
+                grouped_small = tiles["grouped_small", piece]
                 nc.vector.tensor_add(
                     out=grouped_small[:, 2 * SMALL * PACK :], in0=pair_sums[:, 0, :], in1=pair_sums[:, 1, :]
                 )
-                tiles["grouped_small", piece] = grouped_small
 
             def turn(piece, j):
                 raw = tiles["raw", piece]
@@ -229,7 +230,7 @@ def tile_layer_3d_dep_pa_t_kernel(tc, A, P1, P2, P3, P4, a5, gamma, beta, out):
                         nc.tensor.transpose(
                             turned_ps[:, m, h, :], raw[:, j, m, h * P : (h + 1) * P], ident_bf16[:]
                         )
-                turned = twice.tile([P, M, HALVES, P], BF16, name="turned")
+                turned = thrice.tile([P, M, HALVES, P], BF16, name="turned")
                 nc.scalar.copy(
                     out=turned[:].rearrange("p m h c -> p (m h c)").bitcast(F32),
                     in_=turned_ps[:].rearrange("p m h c -> p (m h c)").bitcast(F32),
@@ -253,7 +254,9 @@ def tile_layer_3d_dep_pa_t_kernel(tc, A, P1, P2, P3, P4, a5, gamma, beta, out):
                         )
 
             def round_means(piece):
-                grouped_tr = tiles["grouped_small", piece][:, 0 : 2 * SMALL * PACK].rearrange(
+                grouped_small = once.tile([P, SMALL_COLS * PACK], BF16, align_bytes=64, name="grouped_small")
+                tiles["grouped_small", piece] = grouped_small
+                grouped_tr = grouped_small[:, 0 : 2 * SMALL * PACK].rearrange(
                     "p (s w j) -> p s w j", s=2, j=PACK
                 )
                 for i in range(M // 2):
@@ -419,10 +422,14 @@ def tile_layer_3d_dep_pa_t_kernel(tc, A, P1, P2, P3, P4, a5, gamma, beta, out):
             regroup_a_scalar(0)
             turn(0, 0)
             turn(0, 1)
+            pool(0, 0)
+            turn(0, 2)
+            pool(0, 1)
+            turn(0, 3)
+            pool(0, 2)
             for n, name in enumerate(("p2", "p3", "p4")):
                 group_weight(n + 1, name)
             tiles["raw", 2] = load(2)
-            pool(0, 0)
             for i in range(-1, N_PIECES):
                 ahead, here, behind = i + 1, i, i - 1
                 prepares = ahead < N_PIECES
@@ -437,11 +444,13 @@ def tile_layer_3d_dep_pa_t_kernel(tc, A, P1, P2, P3, P4, a5, gamma, beta, out):
                     scale_a5(ahead)
                     if ahead > 0:
                         regroup_a_scalar(ahead)
-                if prepares:
-                    turn(ahead, 2)
-                    pool(ahead, 1)
                 if multiplies:
                     terms_without_r(here)
+                if turns_next:
+                    turn(ahead + 1, 0)
+                if prepares:
+                    pool(ahead, 3)
+                    round_means(ahead)
                 if prepares:
                     regroup_a_vector(ahead)
                 if multiplies:
@@ -449,9 +458,10 @@ def tile_layer_3d_dep_pa_t_kernel(tc, A, P1, P2, P3, P4, a5, gamma, beta, out):
                     add_out(here, 0)
                 if finishes:
                     activate(behind, 0)
+                if turns_next:
+                    turn(ahead + 1, 1)
+                    pool(ahead + 1, 0)
                 if prepares:
-                    turn(ahead, 3)
-                    pool(ahead, 2)
                     sum_pairs_of_m(ahead)
                     if ahead == 0:
                         finish_weights()
@@ -469,11 +479,10 @@ def tile_layer_3d_dep_pa_t_kernel(tc, A, P1, P2, P3, P4, a5, gamma, beta, out):
                     last_relu_vector(1)
                     last_square(1)
                 if prepares:
-                    pool(ahead, 3)
                     finish_sum_over_m(ahead)
-                    round_means(ahead)
                 if turns_next:
-                    turn(ahead + 1, 0)
+                    turn(ahead + 1, 2)
+                    pool(ahead + 1, 1)
                 if prepares:
                     quantise_means(ahead)
                     quantise_a(ahead)
@@ -485,8 +494,8 @@ def tile_layer_3d_dep_pa_t_kernel(tc, A, P1, P2, P3, P4, a5, gamma, beta, out):
                 if finishes and here != final:
                     activate(behind, 3)
                 if turns_next:
-                    turn(ahead + 1, 1)
-                    pool(ahead + 1, 0)
+                    turn(ahead + 1, 3)
+                    pool(ahead + 1, 2)
                 if multiplies:
                     mix_bank(here, LAST)
 

@@ -34,7 +34,7 @@ POOLED = K_SQUARE * NR
 SMALL_COLS = 2 * SMALL + RUN
 
 UP = 10.0
-STATIONARY = (("p1", 8.0), ("p1", 2.0), ("p2", 1.0 / M), ("p3", 1.0), ("p4", 1.0))
+STATIONARY = (("p1", 8.0), ("p1", 2.0), ("p2", 1.0 / M), ("p3", 1.0), ("p4", 1.0 / 4))
 W_A1_HI, W_A1_LO, W_A2, W_A3, W_A4 = 0, 1, 2, 3, 4
 
 FLOPS = 2 * O * C * B * POSITIONS * (8 + 2 + 1 + 1) // 8
@@ -307,25 +307,11 @@ def tile_layer_3d_dep_pa_t_kernel(tc, A, P1, P2, P3, P4, a5, gamma, beta, out):
                     in_=tiles["grouped_small", piece][:, 2 * SMALL * PACK :],
                 )
 
-            def scale_a5(piece):
+            def terms_without_r(piece):
                 b, kq = divmod(piece, PIECES_PER_B)
                 a5_of_b = a5_sb[:].rearrange("p g x -> p (g x)")[
                     :, b * O_TILES * M * K * NT : (b + 1) * O_TILES * M * K * NT
                 ]
-                a5_scaled = twice.tile([P, O_TILES * M, NT * K_PIECE], F32, name="a5_scaled")
-                nc.gpsimd.tensor_scalar(
-                    out=a5_scaled[:].rearrange("p g (t k) -> p g t k", t=NT),
-                    in0=a5_of_b.rearrange(
-                        "p (g kq k t) -> p kq g t k", kq=PIECES_PER_B, k=K_PIECE, t=NT
-                    )[:, kq],
-                    scalar1=2.0 / 0.5,
-                    scalar2=0.0,
-                    op0=ALU.mult,
-                    op1=ALU.add,
-                )
-                tiles["a5_scaled", piece] = a5_scaled
-
-            def terms_without_r(piece):
                 ar_codes = tiles["small_codes", piece][:, SMALL : 2 * SMALL]
                 ar_scales = small_scales[piece % 2][:, SMALL : 2 * SMALL]
                 a4_acc = psum_small.tile([P, O_TILES * SMALL], F32, tag="small", name="a4_acc")
@@ -336,7 +322,9 @@ def tile_layer_3d_dep_pa_t_kernel(tc, A, P1, P2, P3, P4, a5, gamma, beta, out):
                 nc.vector.tensor_tensor(
                     out=no_r[:].rearrange("p g (t k) -> p g t k", t=NT),
                     in0=a4_acc[:].rearrange("p (g k t) -> p g t k", k=K_PIECE, t=NT),
-                    in1=tiles["a5_scaled", piece][:].rearrange("p g (t k) -> p g t k", t=NT),
+                    in1=a5_of_b.rearrange(
+                        "p (g kq k t) -> p kq g t k", kq=PIECES_PER_B, k=K_PIECE, t=NT
+                    )[:, kq],
                     op=ALU.add,
                 )
                 tiles["no_r", piece] = no_r
@@ -370,7 +358,7 @@ def tile_layer_3d_dep_pa_t_kernel(tc, A, P1, P2, P3, P4, a5, gamma, beta, out):
                     .rearrange("p g x -> p (g x)")
                     .unsqueeze(2)
                     .to_broadcast([P, 2 * NT * K_PIECE, NR]),
-                    scalar=0.5 * UP,
+                    scalar=2.0 * UP,
                     in1=acc[:].rearrange("p i (x r) -> p (i x) r", r=NR),
                     op0=ALU.mult,
                     op1=ALU.add,
@@ -441,7 +429,6 @@ def tile_layer_3d_dep_pa_t_kernel(tc, A, P1, P2, P3, P4, a5, gamma, beta, out):
                 if finishes:
                     add_out(behind, LAST)
                 if prepares:
-                    scale_a5(ahead)
                     if ahead > 0:
                         regroup_a_scalar(ahead)
                 if multiplies:

@@ -168,7 +168,7 @@ def tile_layer_3d_dep_pa_t_kernel(tc, A, P1, P2, P3, P4, a5, gamma, beta, out):
             nc.vector.tensor_copy(out=gamma_beta[:], in_=gb_turned[:, 0 : 2 * O_TILES])
 
         with tc.tile_pool(name="once", bufs=1) as once, tc.tile_pool(name="twice", bufs=2) as twice, tc.tile_pool(
-            name="thrice", bufs=3
+            name="thrice", bufs=4
         ) as thrice:
 
             def mix(acc, weight, ot, codes, scales, start, stop):
@@ -408,13 +408,10 @@ def tile_layer_3d_dep_pa_t_kernel(tc, A, P1, P2, P3, P4, a5, gamma, beta, out):
             assert PACK == O_TILES * (M // 2)
             LAST = PACK - 1
             regroup_a_scalar(0)
-            turn(0, 0)
-            turn(0, 1)
+            for j in range(PACK):
+                turn(0, j)
             pool(0, 0)
-            turn(0, 2)
             pool(0, 1)
-            turn(0, 3)
-            pool(0, 2)
             for n, name in enumerate(("p2", "p3", "p4")):
                 group_weight(n + 1, name)
             tiles["raw", 2] = load(2)
@@ -435,19 +432,18 @@ def tile_layer_3d_dep_pa_t_kernel(tc, A, P1, P2, P3, P4, a5, gamma, beta, out):
                     terms_without_r(here)
                 if turns_next:
                     turn(ahead + 1, 0)
+                    turn(ahead + 1, 1)
                 if prepares:
+                    pool(ahead, 2)
                     pool(ahead, 3)
                     round_means(ahead)
-                if prepares:
                     regroup_a_vector(ahead)
                 if multiplies:
                     mix_bank(here, 0)
                     add_out(here, 0)
                 if finishes:
                     activate(behind, 0)
-                if turns_next:
-                    turn(ahead + 1, 1)
-                    pool(ahead + 1, 0)
+                    activate(behind, 1)
                 if prepares:
                     sum_pairs_of_m(ahead)
                     if ahead == 0:
@@ -458,19 +454,19 @@ def tile_layer_3d_dep_pa_t_kernel(tc, A, P1, P2, P3, P4, a5, gamma, beta, out):
                     mix_bank(here, 1)
                     add_out(here, 1)
                 if finishes:
-                    activate(behind, 1)
                     activate(behind, 2)
                 if here == final:
                     last_relu_scalar(0)
                     last_square(0)
                     last_relu_vector(1)
                     last_square(1)
-                if prepares:
-                    finish_sum_over_m(ahead)
                 if turns_next:
                     turn(ahead + 1, 2)
+                    turn(ahead + 1, 3)
+                    pool(ahead + 1, 0)
                     pool(ahead + 1, 1)
                 if prepares:
+                    finish_sum_over_m(ahead)
                     quantise_means(ahead)
                     quantise_a(ahead)
                     quantise_sum_over_m(ahead)
@@ -480,9 +476,6 @@ def tile_layer_3d_dep_pa_t_kernel(tc, A, P1, P2, P3, P4, a5, gamma, beta, out):
                     add_out(here, 2)
                 if finishes and here != final:
                     activate(behind, 3)
-                if turns_next:
-                    turn(ahead + 1, 3)
-                    pool(ahead + 1, 2)
                 if multiplies:
                     mix_bank(here, LAST)
 

@@ -445,6 +445,8 @@ def tile_layer_3d_dep_pa_t_kernel(tc, A, P1, P2, P3, P4, a5, gamma, beta, out):
                     activate(behind, 0)
                     activate(behind, 1)
                 if prepares:
+                    if ahead > 0:
+                        quantise_means(ahead)
                     sum_pairs_of_m(ahead)
                     if ahead == 0:
                         finish_weights()
@@ -467,7 +469,8 @@ def tile_layer_3d_dep_pa_t_kernel(tc, A, P1, P2, P3, P4, a5, gamma, beta, out):
                     pool(ahead + 1, 1)
                 if prepares:
                     finish_sum_over_m(ahead)
-                    quantise_means(ahead)
+                    if ahead == 0:
+                        quantise_means(ahead)
                     quantise_a(ahead)
                     quantise_sum_over_m(ahead)
                     repeat_scales(ahead)

@@ -37,6 +37,15 @@ UP = 10.0
 STATIONARY = (("p1", 8.0), ("p1", 2.0), ("p2", 1.0 / M), ("p3", 1.0), ("p4", 1.0 / 4))
 W_A1_HI, W_A1_LO, W_A2, W_A3, W_A4 = 0, 1, 2, 3, 4
 
+LATE = 6
+WHOLE = N_PIECES - LATE
+KEPT = LATE + 1
+A4_IN_BANK = 4
+REPS = 3
+Y_SLOTS = N_PIECES + WHOLE
+EARLY = (N_PIECES - 3, N_PIECES - 2)
+ANEW = tuple(range(WHOLE, N_PIECES - REPS))
+
 FLOPS = 2 * O * C * B * POSITIONS * (8 + 2 + 1 + 1) // 8
 
 
@@ -53,17 +62,16 @@ def tile_layer_3d_dep_pa_t_kernel(tc, A, P1, P2, P3, P4, a5, gamma, beta, out):
 
         w_codes = keep.tile([P, len(STATIONARY), O], U32, align_bytes=64)
         w_scales = keep.tile([P, len(STATIONARY), O], U8, align_bytes=64)
-        a5_sb = keep.tile([P, B * O_TILES, M * K * NT], BF16)
         gamma_beta = keep.tile([P, 2 * O_TILES], F32)
-        y = keep.tile([P, O_TILES, N_PIECES, COLS], F32)
+        y = keep.tile([P, Y_SLOTS, COLS], F32)
         sums = keep.tile([P, O_TILES, N_PIECES + 1], F32)
         squares = keep.tile([P, O_TILES, N_PIECES + 1], F32)
         small_scales = [
-            keep.tile([P, SMALL_COLS], U8, align_bytes=64, name="small_scales%d" % parity)
-            for parity in range(2)
+            keep.tile([P, SMALL_COLS], U8, align_bytes=64, name="small_scales%d" % turn_no)
+            for turn_no in range(KEPT)
         ]
-        for parity in range(2):
-            nc.vector.memset(small_scales[parity][:].bitcast(I32), 0)
+        for turn_no in range(KEPT):
+            nc.vector.memset(small_scales[turn_no][:].bitcast(I32), 0)
         ident_bf16 = keep.tile([P, P], BF16)
         make_identity(nc, ident_bf16[:])
         pool_mat = keep.tile([P, 2, POOLED], BF16)
@@ -73,6 +81,7 @@ def tile_layer_3d_dep_pa_t_kernel(tc, A, P1, P2, P3, P4, a5, gamma, beta, out):
         nc.scalar.sqrt(out=table_warmer[:], in_=table_warmer[:])
 
         raw_pool = ctx.enter_context(tc.tile_pool(name="raw_pool", bufs=3))
+        a5_pool = ctx.enter_context(tc.tile_pool(name="a5_pool", bufs=1))
 
         def load(piece):
             b, kq = divmod(piece, PIECES_PER_B)
@@ -85,9 +94,28 @@ def tile_layer_3d_dep_pa_t_kernel(tc, A, P1, P2, P3, P4, a5, gamma, beta, out):
             )
             return raw
 
+        def load_a5(b):
+            a5_sb = a5_pool.tile([P, O_TILES * M * K * NT], BF16, name="a5_sb")
+            nc.sync.dma_start(
+                out=a5_sb[:].rearrange("o (ot x) -> o ot x", ot=O_TILES),
+                in_=a5[b].rearrange("(ot o) m k t -> o ot (m k t)", o=P),
+            )
+            return a5_sb
+
         ctx.enter_context(tc.manual_schedule())
 
         setup = ctx.enter_context(tc.tile_pool(name="setup", bufs=1))
+        once = ctx.enter_context(tc.tile_pool(name="once", bufs=1))
+        rounds = ExitStack()
+        twice = rounds.enter_context(tc.tile_pool(name="twice", bufs=2))
+        thrice = rounds.enter_context(tc.tile_pool(name="thrice", bufs=3))
+        reps = rounds.enter_context(tc.tile_pool(name="reps", bufs=REPS))
+        kept = rounds.enter_context(tc.tile_pool(name="kept", bufs=KEPT))
+        grouped_pairs = []
+        for n in range(2):
+            grouped_pair = kept.tile([P, 2, O * PACK], BF16, align_bytes=64, name="a_codes")
+            grouped_pairs.append(grouped_pair)
+        scaled_pair = kept.tile([P, 2, O * PACK], BF16, align_bytes=64, name="a_codes")
         gb_rows = setup.tile([P, P], BF16, name="gb_rows")
         nc.vector.memset(gb_rows[:], 0.0)
         ident_f32 = setup.tile([P, P], F32, name="ident_f32")
@@ -109,9 +137,7 @@ def tile_layer_3d_dep_pa_t_kernel(tc, A, P1, P2, P3, P4, a5, gamma, beta, out):
         nc.sync.dma_start(
             out=gb_rows[O_TILES : 2 * O_TILES, :], in_=beta.rearrange("(ot o) -> ot o", o=P)
         )
-        nc.sync.dma_start(
-            out=a5_sb[:], in_=a5.rearrange("b (ot o) m k t -> o (b ot) (m k t)", o=P)
-        )
+        first_a5 = load_a5(0)
 
         pool_ones = setup.tile([P, 2, POOLED], F32, name="pool_ones")
         nc.vector.tensor_reduce(
@@ -137,9 +163,9 @@ def tile_layer_3d_dep_pa_t_kernel(tc, A, P1, P2, P3, P4, a5, gamma, beta, out):
             for ot in range(O_TILES):
                 for u in range(2):
                     nc.tensor.transpose(turned[:, ot, u, :], words[:, ot, u, :], ident_f32[:])
-            grouped = setup.tile([P, O * PACK], BF16, name="grouped_" + name, align_bytes=64)
+            grouped = grouped_pairs[n // 2][:, n % 2, :]
             nc.scalar.copy(
-                out=grouped[:].bitcast(F32).rearrange("p (ot o u) -> p ot o u", ot=O_TILES, u=2),
+                out=grouped.bitcast(F32).rearrange("p (ot o u) -> p ot o u", ot=O_TILES, u=2),
                 in_=turned[:].rearrange("p ot u o -> p ot o u"),
             )
             grouped_w[name] = grouped
@@ -148,10 +174,10 @@ def tile_layer_3d_dep_pa_t_kernel(tc, A, P1, P2, P3, P4, a5, gamma, beta, out):
             name, factor = STATIONARY[i]
             scaled = grouped_w[name]
             if factor != 1.0:
-                scaled = setup.tile([P, O * PACK], BF16, name="scaled%d" % (i % 2), align_bytes=64)
-                nc.vector.tensor_scalar_mul(out=scaled[:], in0=grouped_w[name][:], scalar1=factor)
+                scaled = scaled_pair[:, i % 2, :]
+                nc.vector.tensor_scalar_mul(out=scaled, in0=grouped_w[name], scalar1=factor)
             nc.vector.quantize_mx(
-                out=w_codes[:, i, :].bitcast(FP8X4), scales=w_scales[:, i, :], in_=scaled[:]
+                out=w_codes[:, i, :].bitcast(FP8X4), scales=w_scales[:, i, :], in_=scaled
             )
 
         group_weight(0, "p1")
@@ -167,9 +193,7 @@ def tile_layer_3d_dep_pa_t_kernel(tc, A, P1, P2, P3, P4, a5, gamma, beta, out):
             nc.tensor.transpose(gb_turned[:], gb_rows[:], ident_bf16[:])
             nc.vector.tensor_copy(out=gamma_beta[:], in_=gb_turned[:, 0 : 2 * O_TILES])
 
-        with tc.tile_pool(name="once", bufs=1) as once, tc.tile_pool(name="twice", bufs=2) as twice, tc.tile_pool(
-            name="thrice", bufs=4
-        ) as thrice:
+        with rounds:
 
             def mix(acc, weight, ot, codes, scales, start, stop):
                 nc.tensor.matmul_mx(
@@ -183,21 +207,25 @@ def tile_layer_3d_dep_pa_t_kernel(tc, A, P1, P2, P3, P4, a5, gamma, beta, out):
                 )
 
             tiles = {("raw", piece): first_raws[piece] for piece in first_raws}
+            tiles["a5", 0] = first_a5
+            y_of = {(0, piece): y[:, piece, :] for piece in range(N_PIECES)}
+            y_of.update({(1, piece): y[:, N_PIECES + piece, :] for piece in range(WHOLE)})
 
             def regroup_a_scalar(piece):
                 raw = tiles["raw", piece]
                 grouped_a = once.tile([P, COLS, PACK], BF16, align_bytes=64, name="grouped_a")
+                split = M // 2 if piece <= WHOLE else M // 2 - 1
                 target = grouped_a[:].rearrange("p (m th tl x) j -> p th m x j tl", m=M, tl=T_RUN, x=KR)
                 source = raw[:].rearrange("p j m (x th tl) -> p th m x j tl", x=KR, tl=T_RUN)
-                for m in range(M // 2, M):
+                for m in range(split, M):
                     nc.scalar.copy(out=target[:, 1, m], in_=source[:, 1, m])
                 tiles["grouped_a", piece] = grouped_a
-                tiles["regroup_views", piece] = (target, source)
+                tiles["regroup_views", piece] = (target, source, split)
 
             def regroup_a_vector(piece):
-                target, source = tiles["regroup_views", piece]
+                target, source, split = tiles["regroup_views", piece]
                 nc.vector.tensor_copy(out=target[:, 0], in_=source[:, 0])
-                nc.vector.tensor_copy(out=target[:, 1, 0 : M // 2], in_=source[:, 1, 0 : M // 2])
+                nc.vector.tensor_copy(out=target[:, 1, 0:split], in_=source[:, 1, 0:split])
 
             def sum_pairs_of_m(piece):
                 by_m = tiles["grouped_a", piece][:].rearrange("p (m w) j -> p m (w j)", m=M)
@@ -206,8 +234,8 @@ def tile_layer_3d_dep_pa_t_kernel(tc, A, P1, P2, P3, P4, a5, gamma, beta, out):
                 tiles["pair_sums", piece] = pair_sums
 
             def quantise_a(piece):
-                a_codes = twice.tile([P, COLS], U32, align_bytes=64, name="a_codes")
-                a_scales = twice.tile([P, COLS], U8, align_bytes=64, name="a_scales")
+                a_codes = kept.tile([P, COLS], U32, align_bytes=64, name="a_codes")
+                a_scales = kept.tile([P, COLS], U8, align_bytes=64, name="a_scales")
                 nc.vector.quantize_mx(
                     out=a_codes[:].bitcast(FP8X4),
                     scales=a_scales[:],
@@ -266,15 +294,19 @@ def tile_layer_3d_dep_pa_t_kernel(tc, A, P1, P2, P3, P4, a5, gamma, beta, out):
                     )
 
             def quantise_means(piece):
-                small_codes = twice.tile([P, SMALL_COLS], U32, align_bytes=64, name="small_codes")
-                scales = small_scales[piece % 2]
+                small_codes = kept.tile([P, SMALL_COLS], U32, align_bytes=64, name="small_codes")
+                scales = small_scales[piece % KEPT]
                 nc.vector.quantize_mx(
                     out=small_codes[:, 0 : 2 * SMALL].bitcast(FP8X4),
                     scales=scales[:, 0 : 2 * SMALL],
                     in_=tiles["grouped_small", piece][:, 0 : 2 * SMALL * PACK],
                 )
-                at_rep_codes = twice.tile([P, COLS], U32, align_bytes=64, name="at_rep_codes")
-                at_rep_scales = twice.tile([P, COLS], U8, align_bytes=64, name="at_rep_scales")
+                tiles["small_codes", piece] = small_codes
+
+            def repeat_codes(piece):
+                small_codes = tiles["small_codes", piece]
+                at_rep_codes = reps.tile([P, COLS], U32, align_bytes=64, name="at_rep_codes")
+                tiles["at_rep_codes", piece] = at_rep_codes
                 for m in range(M):
                     nc.sync.dma_start(
                         out=at_rep_codes[:, m * RUN : (m + 1) * RUN]
@@ -285,15 +317,13 @@ def tile_layer_3d_dep_pa_t_kernel(tc, A, P1, P2, P3, P4, a5, gamma, beta, out):
                         .unsqueeze(1)
                         .to_broadcast([P, NT, KR]),
                     )
-                tiles["small_codes", piece] = small_codes
-                tiles["at_rep_codes", piece], tiles["at_rep_scales", piece] = at_rep_codes, at_rep_scales
 
             def repeat_scales(piece):
+                at_rep_scales = reps.tile([P, COLS], U8, align_bytes=64, name="at_rep_scales")
+                tiles["at_rep_scales", piece] = at_rep_scales
                 nc.vector.tensor_copy(
-                    out=tiles["at_rep_scales", piece][:]
-                    .bitcast(I32)
-                    .rearrange("p (m t x) -> p m t x", m=M, t=NT),
-                    in_=small_scales[piece % 2][:, 0:SMALL]
+                    out=at_rep_scales[:].bitcast(I32).rearrange("p (m t x) -> p m t x", m=M, t=NT),
+                    in_=small_scales[piece % KEPT][:, 0:SMALL]
                     .bitcast(I32)
                     .rearrange("p (m x) -> p m x", m=M)
                     .unsqueeze(2)
@@ -303,58 +333,79 @@ def tile_layer_3d_dep_pa_t_kernel(tc, A, P1, P2, P3, P4, a5, gamma, beta, out):
             def quantise_sum_over_m(piece):
                 nc.vector.quantize_mx(
                     out=tiles["small_codes", piece][:, 2 * SMALL :].bitcast(FP8X4),
-                    scales=small_scales[piece % 2][:, 2 * SMALL :],
+                    scales=small_scales[piece % KEPT][:, 2 * SMALL :],
                     in_=tiles["grouped_small", piece][:, 2 * SMALL * PACK :],
                 )
 
-            def terms_without_r(piece):
+            def mix_a4(pairs):
+                a4_acc = psum_small.tile([P, len(pairs), SMALL], F32, tag="small", name="a4_acc")
+                for n, (piece, ot) in enumerate(pairs):
+                    mix(
+                        a4_acc[:, n, :], W_A4, ot, tiles["small_codes", piece][:, SMALL : 2 * SMALL],
+                        small_scales[piece % KEPT][:, SMALL : 2 * SMALL], True, True,
+                    )
+                    tiles["a4", piece, ot] = a4_acc[:, n : n + 1, :]
+                if pairs == both_ots(pairs[0][0]):
+                    tiles["a4", pairs[0][0]] = a4_acc[:]
+
+            def both_ots(piece):
+                return [(piece, ot) for ot in range(O_TILES)]
+
+            def terms_without_r(piece, ots):
                 b, kq = divmod(piece, PIECES_PER_B)
-                a5_of_b = a5_sb[:].rearrange("p g x -> p (g x)")[
-                    :, b * O_TILES * M * K * NT : (b + 1) * O_TILES * M * K * NT
-                ]
-                ar_codes = tiles["small_codes", piece][:, SMALL : 2 * SMALL]
-                ar_scales = small_scales[piece % 2][:, SMALL : 2 * SMALL]
-                a4_acc = psum_small.tile([P, O_TILES * SMALL], F32, tag="small", name="a4_acc")
-                for ot in range(O_TILES):
-                    a4_cols = a4_acc[:, ot * SMALL : (ot + 1) * SMALL]
-                    mix(a4_cols, W_A4, ot, ar_codes, ar_scales, True, True)
-                no_r = twice.tile([P, O_TILES * M, NT * K_PIECE], F32, name="no_r")
+                n = len(ots)
+                x_of_ot = M * K * NT
+                a5_of_ots = tiles["a5", b][:, ots[0] * x_of_ot : (ots[0] + n) * x_of_ot]
+                a4 = tiles["a4", piece] if n == O_TILES else tiles["a4", piece, ots[0]]
+                no_r = twice.tile([P, n * M, NT * K_PIECE], F32, name="no_r")
                 nc.vector.tensor_tensor(
                     out=no_r[:].rearrange("p g (t k) -> p g t k", t=NT),
-                    in0=a4_acc[:].rearrange("p (g k t) -> p g t k", k=K_PIECE, t=NT),
-                    in1=a5_of_b.rearrange(
+                    in0=a4.rearrange("p n (m k t) -> p (n m) t k", k=K_PIECE, t=NT),
+                    in1=a5_of_ots.rearrange(
                         "p (g kq k t) -> p kq g t k", kq=PIECES_PER_B, k=K_PIECE, t=NT
                     )[:, kq],
                     op=ALU.add,
                 )
-                tiles["no_r", piece] = no_r
+                for i, ot in enumerate(ots):
+                    tiles["no_r", piece, ot] = no_r[:, i * M : (i + 1) * M, :]
 
-            def mix_bank(piece, bank):
-                ot, m_pair = divmod(bank, M // 2)
-                acc = psum_x.tile([P, 2, RUN], F32, name="acc")
-                am_codes = tiles["small_codes", piece][:, 2 * SMALL :]
-                am_scales = small_scales[piece % 2][:, 2 * SMALL :]
-                for i in range(2):
-                    cols = slice((2 * m_pair + i) * RUN, (2 * m_pair + i + 1) * RUN)
-                    a_codes, a_scales = tiles["a_codes", piece][:, cols], tiles["a_scales", piece][:, cols]
-                    mix(acc[:, i, :], W_A1_HI, ot, a_codes, a_scales, True, False)
-                    mix(acc[:, i, :], W_A1_LO, ot, a_codes, a_scales, False, False)
-                    mix(acc[:, i, :], W_A2, ot, am_codes, am_scales, False, False)
-                    mix(
-                        acc[:, i, :], W_A3, ot, tiles["at_rep_codes", piece][:, cols],
-                        tiles["at_rep_scales", piece][:, cols], False, True,
-                    )
-                tiles["acc", piece, bank] = acc
+            def mix_m(piece, ot, m):
+                m_pair, i = divmod(m, 2)
+                if ("acc", piece, ot, m_pair) not in tiles:
+                    tiles["acc", piece, ot, m_pair] = psum_x.tile([P, 2, RUN], F32, name="acc")
+                acc = tiles["acc", piece, ot, m_pair][:, i, :]
+                cols = slice(m * RUN, (m + 1) * RUN)
+                a_codes, a_scales = tiles["a_codes", piece][:, cols], tiles["a_scales", piece][:, cols]
+                mix(acc, W_A1_HI, ot, a_codes, a_scales, True, False)
+                mix(acc, W_A1_LO, ot, a_codes, a_scales, False, False)
+                mix(
+                    acc, W_A2, ot, tiles["small_codes", piece][:, 2 * SMALL :],
+                    small_scales[piece % KEPT][:, 2 * SMALL :], False, False,
+                )
+                mix(
+                    acc, W_A3, ot, tiles["at_rep_codes", piece][:, cols],
+                    tiles["at_rep_scales", piece][:, cols], False, True,
+                )
 
-            def add_out(piece, bank):
-                ot, m_pair = divmod(bank, M // 2)
-                acc = tiles["acc", piece, bank]
-                g = ot * M + 2 * m_pair
+            def mix_pair(piece, ot, m_pair):
+                mix_m(piece, ot, 2 * m_pair)
+                mix_m(piece, ot, 2 * m_pair + 1)
+
+            def mix_pair_early(piece, m_pair):
+                if m_pair == 0:
+                    bank = psum_turned.tile([P, 2, RUN], F32, name="turned_ps")
+                else:
+                    bank = psum_pooled.tile([P, 2, RUN], F32, name="bank", tag="pooled")
+                tiles["acc", piece, 1, m_pair] = bank
+                mix_pair(piece, 1, m_pair)
+
+            def add_out(piece, ot, m_pair):
+                acc = tiles["acc", piece, ot, m_pair]
                 nc.vector.scalar_tensor_tensor(
-                    out=y[:, ot, piece, 2 * m_pair * RUN : (2 * m_pair + 2) * RUN].rearrange(
+                    out=y_of[ot, piece][:, 2 * m_pair * RUN : (2 * m_pair + 2) * RUN].rearrange(
                         "p (x r) -> p x r", r=NR
                     ),
-                    in0=tiles["no_r", piece][:, g : g + 2, :]
+                    in0=tiles["no_r", piece, ot][:, 2 * m_pair : 2 * m_pair + 2, :]
                     .rearrange("p g x -> p (g x)")
                     .unsqueeze(2)
                     .to_broadcast([P, 2 * NT * K_PIECE, NR]),
@@ -364,123 +415,149 @@ def tile_layer_3d_dep_pa_t_kernel(tc, A, P1, P2, P3, P4, a5, gamma, beta, out):
                     op1=ALU.add,
                 )
 
-            def activate(piece, part):
-                ot, second = divmod(part, 2)
-                y_piece = y[:, ot, piece, :]
-                if not second:
-                    nc.scalar.activation(
-                        out=y_piece, in_=y_piece, func=ACT.Relu,
-                        accum_out=sums[:, ot, piece : piece + 1],
-                    )
-                else:
-                    squared = twice.tile([P, COLS], BF16, name="squared")
-                    nc.scalar.activation(
-                        out=squared[:], in_=y_piece, func=ACT.Square,
-                        accum_out=squares[:, ot, piece : piece + 1],
-                    )
+            def relu(piece, ot):
+                nc.scalar.activation(
+                    out=y_of[ot, piece], in_=y_of[ot, piece], func=ACT.Relu,
+                    accum_out=sums[:, ot, piece : piece + 1],
+                )
 
-            final = N_PIECES - 1
+            def square(piece, ot):
+                squared = once.tile([P, COLS], BF16, name="squared")
+                nc.scalar.activation(
+                    out=squared[:], in_=y_of[ot, piece], func=ACT.Square,
+                    accum_out=squares[:, ot, piece : piece + 1],
+                )
 
-            def last_bank(bank):
-                ot, half = divmod(bank, M // 2)
-                col = final + half
-                part = y[:, ot, final, half * 2 * RUN : (half + 1) * 2 * RUN]
+            def last_half(piece, ot, half):
+                col = (piece, N_PIECES)[half]
+                part = y_of[ot, piece][:, half * 2 * RUN : (half + 1) * 2 * RUN]
                 return part, sums[:, ot, col : col + 1], squares[:, ot, col : col + 1]
 
-            def last_relu_scalar(bank):
-                part, sum_col, square_col = last_bank(bank)
-                nc.scalar.activation(out=part, in_=part, func=ACT.Relu, accum_out=sum_col)
-
-            def last_relu_vector(bank):
-                part, sum_col, square_col = last_bank(bank)
+            def last_relu(piece, ot, half):
+                part, sum_col, square_col = last_half(piece, ot, half)
                 nc.vector.tensor_scalar(
                     out=part, in0=part, scalar1=0.0, scalar2=0.0, op0=ALU.max, op1=ALU.add,
                     accum_out=sum_col,
                 )
 
-            def last_square(bank):
-                part, sum_col, square_col = last_bank(bank)
-                squared = twice.tile([P, COLS], BF16, name="squared")
+            def last_square(piece, ot, half):
+                part, sum_col, square_col = last_half(piece, ot, half)
+                squared = once.tile([P, COLS], BF16, name="squared")
                 nc.scalar.activation(
                     out=squared[:, 0 : 2 * RUN], in_=part, func=ACT.Square, accum_out=square_col
                 )
 
-            assert PACK == O_TILES * (M // 2)
+            assert PACK == M == O_TILES * (M // 2)
             LAST = PACK - 1
+
+            def ots_in_round(piece):
+                return range(O_TILES) if piece < WHOLE else range(1)
+
+            def multiply(piece, unit):
+                if piece < WHOLE:
+                    mix_pair(piece, *divmod(unit, M // 2))
+                else:
+                    mix_m(piece, 0, unit)
+
+            def empty(piece, unit):
+                if piece < WHOLE:
+                    add_out(piece, *divmod(unit, M // 2))
+                elif unit % 2 == 1:
+                    add_out(piece, 0, unit // 2)
+
             regroup_a_scalar(0)
-            for j in range(PACK):
-                turn(0, j)
+            turn(0, 0)
+            turn(0, 1)
+            group_weight(1, "p2")
+            group_weight(2, "p3")
             pool(0, 0)
+            turn(0, 2)
             pool(0, 1)
-            for n, name in enumerate(("p2", "p3", "p4")):
-                group_weight(n + 1, name)
+            turn(0, 3)
+            pool(0, 2)
+            group_weight(3, "p4")
             tiles["raw", 2] = load(2)
+            final = N_PIECES - 1
             for i in range(-1, N_PIECES):
                 ahead, here, behind = i + 1, i, i - 1
                 prepares = ahead < N_PIECES
                 turns_next = ahead + 1 < N_PIECES
-                multiplies = 0 <= here < N_PIECES
-                finishes = 0 <= behind < N_PIECES
+                multiplies = here >= 0
+                finishes = behind >= 0
+                both = 0 <= behind < WHOLE
                 if 3 <= ahead + 2 < N_PIECES:
                     tiles["raw", ahead + 2] = load(ahead + 2)
                 if finishes:
-                    add_out(behind, LAST)
-                if prepares:
-                    if ahead > 0:
-                        regroup_a_scalar(ahead)
+                    empty(behind, LAST)
                 if multiplies:
-                    terms_without_r(here)
+                    mix_a4([(here, ot) for ot in ots_in_round(here)])
+                    terms_without_r(here, ots_in_round(here))
+                if ahead == PIECES_PER_B:
+                    tiles["a5", 1] = load_a5(1)
+                if here == final:
+                    for piece in ANEW[: len(EARLY)]:
+                        repeat_scales(piece)
+                if 0 < ahead < N_PIECES:
+                    regroup_a_scalar(ahead)
                 if turns_next:
                     turn(ahead + 1, 0)
-                    turn(ahead + 1, 1)
                 if prepares:
-                    pool(ahead, 2)
                     pool(ahead, 3)
                     round_means(ahead)
                     regroup_a_vector(ahead)
                 if multiplies:
-                    mix_bank(here, 0)
-                    add_out(here, 0)
+                    multiply(here, 0)
+                    empty(here, 0)
                 if finishes:
-                    activate(behind, 0)
-                    activate(behind, 1)
+                    relu(behind, 0)
+                if turns_next:
+                    turn(ahead + 1, 1)
+                    pool(ahead + 1, 0)
                 if prepares:
-                    if ahead > 0:
-                        quantise_means(ahead)
                     sum_pairs_of_m(ahead)
-                    if ahead == 0:
-                        finish_weights()
-                    if ahead == 2:
-                        turn_gamma_beta()
+                if 0 < ahead < N_PIECES:
+                    quantise_means(ahead)
+                    repeat_codes(ahead)
+                if ahead == 0:
+                    finish_weights()
+                if ahead == 2:
+                    turn_gamma_beta()
                 if multiplies:
-                    mix_bank(here, 1)
-                    add_out(here, 1)
-                if finishes:
-                    activate(behind, 2)
-                if here == final:
-                    last_relu_scalar(0)
-                    last_square(0)
-                    last_relu_vector(1)
-                    last_square(1)
+                    multiply(here, 1)
+                    empty(here, 1)
+                if both:
+                    square(behind, 0)
+                    relu(behind, 1)
                 if turns_next:
                     turn(ahead + 1, 2)
-                    turn(ahead + 1, 3)
-                    pool(ahead + 1, 0)
                     pool(ahead + 1, 1)
+                if ahead == 0:
+                    quantise_means(ahead)
+                    repeat_codes(ahead)
                 if prepares:
                     finish_sum_over_m(ahead)
-                    if ahead == 0:
-                        quantise_means(ahead)
                     quantise_a(ahead)
                     quantise_sum_over_m(ahead)
                     repeat_scales(ahead)
                 if multiplies:
-                    mix_bank(here, 2)
-                    add_out(here, 2)
-                if finishes and here != final:
-                    activate(behind, 3)
+                    multiply(here, 2)
+                if multiplies and here < final:
+                    empty(here, 2)
+                if both:
+                    square(behind, 1)
+                elif finishes:
+                    square(behind, 0)
+                if turns_next:
+                    turn(ahead + 1, 3)
+                    pool(ahead + 1, 2)
                 if multiplies:
-                    mix_bank(here, LAST)
+                    multiply(here, LAST)
+                if here == final - 1:
+                    for piece in EARLY:
+                        for m_pair in range(M // 2):
+                            mix_pair_early(piece, m_pair)
+                    for piece in ANEW[: len(EARLY)]:
+                        repeat_codes(piece)
 
             count = float(B * POSITIONS)
             total = keep.tile([P, O_TILES], F32)
@@ -507,6 +584,7 @@ def tile_layer_3d_dep_pa_t_kernel(tc, A, P1, P2, P3, P4, a5, gamma, beta, out):
                     out=var[:, col], in0=var[:, col], scalar1=0.0, scalar2=BN_EPS * UP * UP,
                     op0=ALU.max, op1=ALU.add,
                 )
+                nc.scalar.sqrt(out=std[:, col], in_=var[:, col])
 
             def gain_and_shift(ot):
                 col = slice(ot, ot + 1)
@@ -520,51 +598,93 @@ def tile_layer_3d_dep_pa_t_kernel(tc, A, P1, P2, P3, P4, a5, gamma, beta, out):
                     out=shift[:, col], in0=gamma_beta[:, O_TILES + ot : O_TILES + ot + 1], in1=shift[:, col]
                 )
 
-            def normalise(ot, step, staged):
+            def normalise(ot, step, staged, groups, engine):
                 b, m = divmod(step, M)
-                source = y[
-                    :, ot, b * PIECES_PER_B : (b + 1) * PIECES_PER_B, m * RUN : (m + 1) * RUN
-                ].rearrange("p q (th tl x) -> p th q x tl", tl=T_RUN, x=KR)
-                target = staged[:].rearrange("p q x (th tl) -> p th q x tl", tl=T_RUN)
-                for th in range(NT // T_RUN):
-                    if step % 2 == 0:
-                        nc.vector.tensor_scalar(
-                            out=target[:, th], in0=source[:, th], scalar1=gain[:, ot : ot + 1],
-                            scalar2=shift[:, ot : ot + 1], op0=ALU.mult, op1=ALU.add,
-                        )
-                    else:
-                        nc.scalar.activation(
-                            out=target[:, th], in_=source[:, th], func=ACT.Identity,
-                            bias=shift[:, ot : ot + 1], scale=gain[:, ot : ot + 1],
-                        )
+                for view, first in groups:
+                    n = view.shape[1]
+                    q = first - b * PIECES_PER_B
+                    source = view[:, :, m * RUN : (m + 1) * RUN].rearrange(
+                        "p q (th tl x) -> p th q x tl", tl=T_RUN, x=KR
+                    )
+                    target = staged[:, q : q + n].rearrange("p q x (th tl) -> p th q x tl", tl=T_RUN)
+                    for th in range(NT // T_RUN):
+                        if engine is not nc.scalar:
+                            engine.tensor_scalar(
+                                out=target[:, th], in0=source[:, th], scalar1=gain[:, ot : ot + 1],
+                                scalar2=shift[:, ot : ot + 1], op0=ALU.mult, op1=ALU.add,
+                            )
+                        else:
+                            nc.scalar.activation(
+                                out=target[:, th], in_=source[:, th], func=ACT.Identity,
+                                bias=shift[:, ot : ot + 1], scale=gain[:, ot : ot + 1],
+                            )
                 nc.sync.dma_start(
                     out=out[b].rearrange("(ot o) m k r t -> o ot m (k r t)", o=P)[:, ot, m, :],
                     in_=staged[:].rearrange("p q x t -> p (q x t)"),
                 )
 
-            def stage_in_raw_buffer():
-                return raw_pool.tile([P, PIECES_PER_B, KR, NT], F32, name="raw")
+            def normalise_0(step, engine):
+                first = step // M * PIECES_PER_B
+                normalise(
+                    0, step, raw_pool.tile([P, PIECES_PER_B, KR, NT], F32, name="raw"),
+                    [(y[:, first : first + PIECES_PER_B, :], first)], engine,
+                )
 
-            variance(0)
-            nc.scalar.sqrt(out=std[:, 0:1], in_=var[:, 0:1])
-            add_out(final, LAST)
-            gain_and_shift(0)
-            normalise(0, 0, stage_in_raw_buffer())
-            normalise(0, 1, stage_in_raw_buffer())
-            activate(final - 1, 3)
-            for bank in (2, 3):
-                last_relu_vector(bank)
-                last_square(bank)
-            normalise(0, 2, stage_in_raw_buffer())
+            order = EARLY + (N_PIECES - 1,) + ANEW
+            late_a = once.tile([P, 2, COLS], F32, align_bytes=64, name="grouped_a")
+            late_b = once.tile([P, 2, COLS], F32, name="pair_sums")
+            late_groups = [(y[:, 0:2, :], WHOLE), (late_b[:], WHOLE + 2), (late_a[:], WHOLE + 4)]
+            for view, first in late_groups:
+                for n in range(2):
+                    y_of[1, first + n] = view[:, n, :]
+
+            last_relu(final, 0, 0)
+            last_square(final, 0, 0)
+            add_out(final, 0, 1)
+            last_relu(final, 0, 1)
+            last_square(final, 0, 1)
+            for n, piece in enumerate(order):
+                last = n == LATE - 1
+                if n % A4_IN_BANK == 0:
+                    mix_a4([(late, 1) for late in order[n : n + A4_IN_BANK]])
+                terms_without_r(piece, range(1, 2))
+                if piece not in EARLY:
+                    mix_pair(piece, 1, 0)
+                    mix_pair(piece, 1, 1)
+                if piece == final:
+                    repeat_codes(ANEW[-1])
+                add_out(piece, 1, 0)
+                if n == 0:
+                    variance(0)
+                    add_out(piece, 1, 1)
+                    gain_and_shift(0)
+                if last:
+                    last_relu(piece, 1, 0)
+                    last_square(piece, 1, 0)
+                if n == 0:
+                    normalise_0(0, nc.vector)
+                    normalise_0(1, nc.scalar)
+                else:
+                    normalise_0(n + 1, nc.vector)
+                if n > 0:
+                    add_out(piece, 1, 1)
+                if piece == final:
+                    repeat_scales(ANEW[-1])
+                if last:
+                    last_relu(piece, 1, 1)
+                    last_square(piece, 1, 1)
+                    normalise_0(7, nc.vector)
+                else:
+                    relu(piece, 1)
+                    square(piece, 1)
             variance(1)
-            normalise(0, 3, stage_in_raw_buffer())
-            nc.scalar.sqrt(out=std[:, 1:2], in_=var[:, 1:2])
-            normalise(0, 4, stage_in_raw_buffer())
             gain_and_shift(1)
-            for step in range(5, B * M):
-                normalise(0, step, stage_in_raw_buffer())
 
         staged_pool = ctx.enter_context(tc.tile_pool(name="staged_pool", bufs=4))
+        whole_groups = [
+            [(y[:, N_PIECES : N_PIECES + PIECES_PER_B, :], 0)],
+            [(y[:, N_PIECES + PIECES_PER_B :, :], PIECES_PER_B)] + late_groups,
+        ]
         for step in range(B * M):
             staged = staged_pool.tile([P, PIECES_PER_B, KR, NT], F32)
-            normalise(1, step, staged)
+            normalise(1, step, staged, whole_groups[step // M], nc.vector if step % 2 == 0 else nc.scalar)

@@ -86,12 +86,14 @@ def tile_layer_3d_dep_pa_t_kernel(tc, A, P1, P2, P3, P4, a5, gamma, beta, out):
         def load(piece):
             b, kq = divmod(piece, PIECES_PER_B)
             raw = raw_pool.tile([P, PACK, M, RUN], BF16, name="raw")
-            nc.sync.dma_start(
-                out=raw[:],
-                in_=A[b].rearrange("(p j) m k r t -> p j m (k r t)", j=PACK)[
-                    :, :, :, kq * RUN : (kq + 1) * RUN
-                ],
-            )
+            source = A[b].rearrange("(p j) m k r t -> p j m (k r t)", j=PACK)[
+                :, :, :, kq * RUN : (kq + 1) * RUN
+            ]
+            if piece == 0:
+                for m in range(M):
+                    nc.sync.dma_start(out=raw[:, :, m], in_=source[:, :, m])
+            else:
+                nc.sync.dma_start(out=raw[:], in_=source)
             return raw
 
         def load_a5(b):
@@ -214,18 +216,23 @@ def tile_layer_3d_dep_pa_t_kernel(tc, A, P1, P2, P3, P4, a5, gamma, beta, out):
             def regroup_a_scalar(piece):
                 raw = tiles["raw", piece]
                 grouped_a = once.tile([P, COLS, PACK], BF16, align_bytes=64, name="grouped_a")
-                split = M // 2 if piece <= WHOLE else M // 2 - 1
+                split = KR * 3 // 8 if piece <= WHOLE + 1 else KR // 4
                 target = grouped_a[:].rearrange("p (m th tl x) j -> p th m x j tl", m=M, tl=T_RUN, x=KR)
                 source = raw[:].rearrange("p j m (x th tl) -> p th m x j tl", x=KR, tl=T_RUN)
-                for m in range(split, M):
-                    nc.scalar.copy(out=target[:, 1, m], in_=source[:, 1, m])
+                for m in range(M):
+                    nc.scalar.copy(out=target[:, 1, m, split:], in_=source[:, 1, m, split:])
                 tiles["grouped_a", piece] = grouped_a
                 tiles["regroup_views", piece] = (target, source, split)
 
             def regroup_a_vector(piece):
                 target, source, split = tiles["regroup_views", piece]
-                nc.vector.tensor_copy(out=target[:, 0], in_=source[:, 0])
-                nc.vector.tensor_copy(out=target[:, 1, 0:split], in_=source[:, 1, 0:split])
+                if piece == 0:
+                    for m in range(M):
+                        nc.vector.tensor_copy(out=target[:, 0, m], in_=source[:, 0, m])
+                        nc.vector.tensor_copy(out=target[:, 1, m, 0:split], in_=source[:, 1, m, 0:split])
+                else:
+                    nc.vector.tensor_copy(out=target[:, 0], in_=source[:, 0])
+                    nc.vector.tensor_copy(out=target[:, 1, :, 0:split], in_=source[:, 1, :, 0:split])
 
             def sum_pairs_of_m(piece):
                 by_m = tiles["grouped_a", piece][:].rearrange("p (m w) j -> p m (w j)", m=M)

@@ -216,7 +216,7 @@ def tile_layer_3d_dep_pa_t_kernel(tc, A, P1, P2, P3, P4, a5, gamma, beta, out):
             def regroup_a_scalar(piece):
                 raw = tiles["raw", piece]
                 grouped_a = once.tile([P, COLS, PACK], BF16, align_bytes=64, name="grouped_a")
-                split = KR * 3 // 8 if piece <= WHOLE + 1 else KR // 4
+                split = KR // 4 if piece <= WHOLE + 1 else KR // 8
                 target = grouped_a[:].rearrange("p (m th tl x) j -> p th m x j tl", m=M, tl=T_RUN, x=KR)
                 source = raw[:].rearrange("p j m (x th tl) -> p th m x j tl", x=KR, tl=T_RUN)
                 for m in range(M):

@@ -40,7 +40,6 @@ W_A1_HI, W_A1_LO, W_A2, W_A3, W_A4 = 0, 1, 2, 3, 4
 LATE = 6
 WHOLE = N_PIECES - LATE
 KEPT = LATE + 1
-A4_IN_BANK = 4
 REPS = 3
 Y_SLOTS = N_PIECES + WHOLE
 EARLY = (N_PIECES - 3, N_PIECES - 2)
@@ -216,7 +215,7 @@ def tile_layer_3d_dep_pa_t_kernel(tc, A, P1, P2, P3, P4, a5, gamma, beta, out):
             def regroup_a_scalar(piece):
                 raw = tiles["raw", piece]
                 grouped_a = once.tile([P, COLS, PACK], BF16, align_bytes=64, name="grouped_a")
-                split = KR // 4 if piece <= WHOLE + 1 else KR // 8
+                split = KR * 5 // 16 if piece <= WHOLE + 1 else KR * 3 // 16
                 target = grouped_a[:].rearrange("p (m th tl x) j -> p th m x j tl", m=M, tl=T_RUN, x=KR)
                 source = raw[:].rearrange("p j m (x th tl) -> p th m x j tl", x=KR, tl=T_RUN)
                 for m in range(M):
@@ -395,8 +394,23 @@ def tile_layer_3d_dep_pa_t_kernel(tc, A, P1, P2, P3, P4, a5, gamma, beta, out):
                 )
 
             def mix_pair(piece, ot, m_pair):
-                mix_m(piece, ot, 2 * m_pair)
-                mix_m(piece, ot, 2 * m_pair + 1)
+                if ("acc", piece, ot, m_pair) not in tiles:
+                    tiles["acc", piece, ot, m_pair] = psum_x.tile([P, 2, RUN], F32, name="acc")
+                acc = tiles["acc", piece, ot, m_pair]
+                bank = acc[:].rearrange("p i x -> p (i x)")
+                cols = slice(2 * m_pair * RUN, (2 * m_pair + 2) * RUN)
+                a_codes, a_scales = tiles["a_codes", piece][:, cols], tiles["a_scales", piece][:, cols]
+                mix(bank, W_A1_HI, ot, a_codes, a_scales, True, False)
+                mix(bank, W_A1_LO, ot, a_codes, a_scales, False, False)
+                for i in range(2):
+                    mix(
+                        acc[:, i, :], W_A2, ot, tiles["small_codes", piece][:, 2 * SMALL :],
+                        small_scales[piece % KEPT][:, 2 * SMALL :], False, False,
+                    )
+                mix(
+                    bank, W_A3, ot, tiles["at_rep_codes", piece][:, cols],
+                    tiles["at_rep_scales", piece][:, cols], False, True,
+                )
 
             def mix_pair_early(piece, m_pair):
                 if m_pair == 0:
@@ -485,6 +499,7 @@ def tile_layer_3d_dep_pa_t_kernel(tc, A, P1, P2, P3, P4, a5, gamma, beta, out):
             group_weight(3, "p4")
             tiles["raw", 2] = load(2)
             final = N_PIECES - 1
+            order = EARLY + (final,) + ANEW
             for i in range(-1, N_PIECES):
                 ahead, here, behind = i + 1, i, i - 1
                 prepares = ahead < N_PIECES
@@ -496,8 +511,11 @@ def tile_layer_3d_dep_pa_t_kernel(tc, A, P1, P2, P3, P4, a5, gamma, beta, out):
                     tiles["raw", ahead + 2] = load(ahead + 2)
                 if finishes:
                     empty(behind, LAST)
-                if multiplies:
+                if here == final:
+                    mix_a4([(final, 0)] + [(piece, 1) for piece in order[:3]])
+                elif multiplies:
                     mix_a4([(here, ot) for ot in ots_in_round(here)])
+                if multiplies:
                     terms_without_r(here, ots_in_round(here))
                 if ahead == PIECES_PER_B:
                     tiles["a5", 1] = load_a5(1)
@@ -637,7 +655,6 @@ def tile_layer_3d_dep_pa_t_kernel(tc, A, P1, P2, P3, P4, a5, gamma, beta, out):
                     [(y[:, first : first + PIECES_PER_B, :], first)], engine,
                 )
 
-            order = EARLY + (N_PIECES - 1,) + ANEW
             late_a = once.tile([P, 2, COLS], F32, align_bytes=64, name="grouped_a")
             late_b = once.tile([P, 2, COLS], F32, name="pair_sums")
             late_groups = [(y[:, 0:2, :], WHOLE), (late_b[:], WHOLE + 2), (late_a[:], WHOLE + 4)]
@@ -645,29 +662,29 @@ def tile_layer_3d_dep_pa_t_kernel(tc, A, P1, P2, P3, P4, a5, gamma, beta, out):
                 for n in range(2):
                     y_of[1, first + n] = view[:, n, :]
 
+            terms_without_r(order[0], range(1, 2))
             last_relu(final, 0, 0)
             last_square(final, 0, 0)
             add_out(final, 0, 1)
+            terms_without_r(order[1], range(1, 2))
             last_relu(final, 0, 1)
             last_square(final, 0, 1)
             for n, piece in enumerate(order):
                 last = n == LATE - 1
-                if n % A4_IN_BANK == 0:
-                    mix_a4([(late, 1) for late in order[n : n + A4_IN_BANK]])
-                terms_without_r(piece, range(1, 2))
                 if piece not in EARLY:
                     mix_pair(piece, 1, 0)
                     mix_pair(piece, 1, 1)
                 if piece == final:
                     repeat_codes(ANEW[-1])
                 add_out(piece, 1, 0)
+                if n == 2:
+                    mix_a4([(late, 1) for late in order[3:]])
+                if 0 < n < LATE - 1:
+                    terms_without_r(order[n + 1], range(1, 2))
                 if n == 0:
                     variance(0)
                     add_out(piece, 1, 1)
                     gain_and_shift(0)
-                if last:
-                    last_relu(piece, 1, 0)
-                    last_square(piece, 1, 0)
                 if n == 0:
                     normalise_0(0, nc.vector)
                     normalise_0(1, nc.scalar)
@@ -678,9 +695,10 @@ def tile_layer_3d_dep_pa_t_kernel(tc, A, P1, P2, P3, P4, a5, gamma, beta, out):
                 if piece == final:
                     repeat_scales(ANEW[-1])
                 if last:
-                    last_relu(piece, 1, 1)
-                    last_square(piece, 1, 1)
-                    normalise_0(7, nc.vector)
+                    for half in range(2):
+                        last_relu(piece, 1, half)
+                        last_square(piece, 1, half)
+                    normalise_0(n + 2, nc.vector)
                 else:
                     relu(piece, 1)
                     square(piece, 1)

@@ -218,8 +218,11 @@ def tile_layer_3d_dep_pa_t_kernel(tc, A, P1, P2, P3, P4, a5, gamma, beta, out):
                 split = KR * 5 // 16 if piece <= WHOLE + 1 else KR * 3 // 16
                 target = grouped_a[:].rearrange("p (m th tl x) j -> p th m x j tl", m=M, tl=T_RUN, x=KR)
                 source = raw[:].rearrange("p j m (x th tl) -> p th m x j tl", x=KR, tl=T_RUN)
-                for m in range(M):
-                    nc.scalar.copy(out=target[:, 1, m, split:], in_=source[:, 1, m, split:])
+                if piece == 0:
+                    for m in range(M):
+                        nc.scalar.copy(out=target[:, 1, m, split:], in_=source[:, 1, m, split:])
+                else:
+                    nc.scalar.copy(out=target[:, 1, :, split:], in_=source[:, 1, :, split:])
                 tiles["grouped_a", piece] = grouped_a
                 tiles["regroup_views", piece] = (target, source, split)
 
@@ -323,6 +326,18 @@ def tile_layer_3d_dep_pa_t_kernel(tc, A, P1, P2, P3, P4, a5, gamma, beta, out):
                         .unsqueeze(1)
                         .to_broadcast([P, NT, KR]),
                     )
+
+            def repeat_codes_vector(piece):
+                at_rep_codes = reps.tile([P, COLS], U32, align_bytes=64, name="at_rep_codes")
+                nc.vector.tensor_copy(
+                    out=at_rep_codes[:].bitcast(I32).rearrange("p (m t x) -> p m t x", m=M, t=NT),
+                    in_=tiles["small_codes", piece][:, 0:SMALL]
+                    .bitcast(I32)
+                    .rearrange("p (m x) -> p m x", m=M)
+                    .unsqueeze(2)
+                    .to_broadcast([P, M, NT, KR]),
+                )
+                tiles["at_rep_codes", piece] = at_rep_codes
 
             def repeat_scales(piece):
                 at_rep_scales = reps.tile([P, COLS], U8, align_bytes=64, name="at_rep_scales")
@@ -587,6 +602,7 @@ def tile_layer_3d_dep_pa_t_kernel(tc, A, P1, P2, P3, P4, a5, gamma, beta, out):
             count = float(B * POSITIONS)
             total = keep.tile([P, O_TILES], F32)
             total_sq = keep.tile([P, O_TILES], F32)
+            minus_mean = keep.tile([P, O_TILES], F32)
             mean_sq = keep.tile([P, O_TILES], F32)
             var = keep.tile([P, O_TILES], F32)
             std = keep.tile([P, O_TILES], F32)
@@ -596,11 +612,9 @@ def tile_layer_3d_dep_pa_t_kernel(tc, A, P1, P2, P3, P4, a5, gamma, beta, out):
             def variance(ot):
                 col = slice(ot, ot + 1)
                 nc.vector.tensor_reduce(out=total[:, col], in_=sums[:, ot, :], axis=AXIS_X, op=ALU.add)
+                nc.vector.tensor_scalar_mul(out=minus_mean[:, col], in0=total[:, col], scalar1=-1.0 / count)
+                nc.vector.tensor_mul(out=mean_sq[:, col], in0=minus_mean[:, col], in1=minus_mean[:, col])
                 nc.vector.tensor_reduce(out=total_sq[:, col], in_=squares[:, ot, :], axis=AXIS_X, op=ALU.add)
-                nc.vector.scalar_tensor_tensor(
-                    out=mean_sq[:, col], in0=total[:, col], scalar=1.0 / (count * count), in1=total[:, col],
-                    op0=ALU.mult, op1=ALU.mult,
-                )
                 nc.vector.scalar_tensor_tensor(
                     out=var[:, col], in0=total_sq[:, col], scalar=1.0 / count, in1=mean_sq[:, col],
                     op0=ALU.mult, op1=ALU.subtract,
@@ -616,15 +630,13 @@ def tile_layer_3d_dep_pa_t_kernel(tc, A, P1, P2, P3, P4, a5, gamma, beta, out):
                 nc.vector.reciprocal(out=gain[:, col], in_=std[:, col])
                 nc.vector.tensor_mul(out=gain[:, col], in0=gain[:, col], in1=gamma_beta[:, col])
                 nc.vector.scalar_tensor_tensor(
-                    out=shift[:, col], in0=total[:, col], scalar=1.0 / count, in1=gain[:, col],
-                    op0=ALU.mult, op1=ALU.mult,
-                )
-                nc.vector.tensor_sub(
-                    out=shift[:, col], in0=gamma_beta[:, O_TILES + ot : O_TILES + ot + 1], in1=shift[:, col]
+                    out=shift[:, col], in0=gain[:, col], scalar=minus_mean[:, col],
+                    in1=gamma_beta[:, O_TILES + ot : O_TILES + ot + 1], op0=ALU.mult, op1=ALU.add,
                 )
 
             def normalise(ot, step, staged, groups, engine):
                 b, m = divmod(step, M)
+                stored = 0
                 for view, first in groups:
                     n = view.shape[1]
                     q = first - b * PIECES_PER_B
@@ -643,16 +655,22 @@ def tile_layer_3d_dep_pa_t_kernel(tc, A, P1, P2, P3, P4, a5, gamma, beta, out):
                                 out=target[:, th], in_=source[:, th], func=ACT.Identity,
                                 bias=shift[:, ot : ot + 1], scale=gain[:, ot : ot + 1],
                             )
-                nc.sync.dma_start(
-                    out=out[b].rearrange("(ot o) m k r t -> o ot m (k r t)", o=P)[:, ot, m, :],
-                    in_=staged[:].rearrange("p q x t -> p (q x t)"),
-                )
+                    done = q + n
+                    if step == 0 and ot == 0 or done == PIECES_PER_B:
+                        nc.sync.dma_start(
+                            out=out[b].rearrange("(ot o) m k r t -> o ot m (k r t)", o=P)[
+                                :, ot, m, stored * RUN : done * RUN
+                            ],
+                            in_=staged[:, stored:done].rearrange("p q x t -> p (q x t)"),
+                        )
+                        stored = done
 
             def normalise_0(step, engine):
                 first = step // M * PIECES_PER_B
+                n = PIECES_PER_B // 2 if step == 0 else PIECES_PER_B
                 normalise(
                     0, step, raw_pool.tile([P, PIECES_PER_B, KR, NT], F32, name="raw"),
-                    [(y[:, first : first + PIECES_PER_B, :], first)], engine,
+                    [(y[:, q : q + n, :], q) for q in range(first, first + PIECES_PER_B, n)], engine,
                 )
 
             late_a = once.tile([P, 2, COLS], F32, align_bytes=64, name="grouped_a")
@@ -674,8 +692,6 @@ def tile_layer_3d_dep_pa_t_kernel(tc, A, P1, P2, P3, P4, a5, gamma, beta, out):
                 if piece not in EARLY:
                     mix_pair(piece, 1, 0)
                     mix_pair(piece, 1, 1)
-                if piece == final:
-                    repeat_codes(ANEW[-1])
                 add_out(piece, 1, 0)
                 if n == 2:
                     mix_a4([(late, 1) for late in order[3:]])
@@ -689,10 +705,11 @@ def tile_layer_3d_dep_pa_t_kernel(tc, A, P1, P2, P3, P4, a5, gamma, beta, out):
                     normalise_0(0, nc.vector)
                     normalise_0(1, nc.scalar)
                 else:
-                    normalise_0(n + 1, nc.vector)
+                    normalise_0(n + 1, nc.gpsimd if n == 3 else nc.vector)
                 if n > 0:
                     add_out(piece, 1, 1)
                 if piece == final:
+                    repeat_codes_vector(ANEW[-1])
                     repeat_scales(ANEW[-1])
                 if last:
                     for half in range(2):

from contextlib import ExitStack

import concourse.mybir as mybir
from concourse.masks import make_identity

BF16 = mybir.dt.bfloat16
F32 = mybir.dt.float32
I32 = mybir.dt.int32
U32 = mybir.dt.uint32
U8 = mybir.dt.uint8
FP8X4 = mybir.dt.float8_e4m3fn_x4
ALU = mybir.AluOpType
ACT = mybir.ActivationFunctionType
AXIS_X = mybir.AxisListType.X

B, C, O, M, K, NR, NT = 2, 512, 256, 4, 32, 8, 8
BN_EPS = 1e-5
P = 128
PACK = 4
O_TILES = O // P
POSITIONS = M * K * NR * NT

K_PIECE = 4
PIECES_PER_B = K // K_PIECE
N_PIECES = B * PIECES_PER_B
KR = K_PIECE * NR
RUN = K_PIECE * NR * NT
COLS = M * RUN
SMALL = M * KR
HALVES = RUN // P
K_SQUARE = K_PIECE // HALVES
T_RUN = NT // 2
POOLED = K_SQUARE * NR
SMALL_COLS = 2 * SMALL + RUN

UP = 10.0
STATIONARY = (("p1", 8.0), ("p1", 2.0), ("p2", 1.0 / M), ("p3", 1.0), ("p4", 1.0 / 4))
W_A1_HI, W_A1_LO, W_A2, W_A3, W_A4 = 0, 1, 2, 3, 4

LATE = 6
WHOLE = N_PIECES - LATE
KEPT = LATE + 1
REPS = 3
Y_SLOTS = N_PIECES + WHOLE
EARLY = (N_PIECES - 3, N_PIECES - 2)
ANEW = tuple(range(WHOLE, N_PIECES - REPS))

FLOPS = 2 * O * C * B * POSITIONS * (8 + 2 + 1 + 1) // 8


def tile_layer_3d_dep_pa_t_kernel(tc, A, P1, P2, P3, P4, a5, gamma, beta, out):
    nc = tc.nc
    weights = {"p1": P1, "p2": P2, "p3": P3, "p4": P4}

    with ExitStack() as ctx:
        keep = ctx.enter_context(tc.tile_pool(name="keep", bufs=1))
        psum_x = ctx.enter_context(tc.psum_pool(name="psum_x", bufs=3))
        psum_turned = ctx.enter_context(tc.psum_pool(name="psum_turned", bufs=2))
        psum_pooled = ctx.enter_context(tc.psum_pool(name="psum_pooled", bufs=2))
        psum_small = ctx.enter_context(tc.psum_pool(name="psum_small", bufs=1))

        w_codes = keep.tile([P, len(STATIONARY), O], U32, align_bytes=64)
        w_scales = keep.tile([P, len(STATIONARY), O], U8, align_bytes=64)
        gamma_beta = keep.tile([P, 2 * O_TILES], F32)
        y = keep.tile([P, Y_SLOTS, COLS], F32)
        sums = keep.tile([P, O_TILES, N_PIECES + 1], F32)
        squares = keep.tile([P, O_TILES, N_PIECES + 1], F32)
        small_scales = [
            keep.tile([P, SMALL_COLS], U8, align_bytes=64, name="small_scales%d" % turn_no)
            for turn_no in range(KEPT)
        ]
        for turn_no in range(KEPT):
            nc.vector.memset(small_scales[turn_no][:].bitcast(I32), 0)
        ident_bf16 = keep.tile([P, P], BF16)
        make_identity(nc, ident_bf16[:])
        pool_mat = keep.tile([P, 2, POOLED], BF16)

        table_warmer = keep.tile([P, 1], F32)
        nc.vector.memset(table_warmer[:], 1.0)
        nc.scalar.sqrt(out=table_warmer[:], in_=table_warmer[:])

        raw_pool = ctx.enter_context(tc.tile_pool(name="raw_pool", bufs=3))
        a5_pool = ctx.enter_context(tc.tile_pool(name="a5_pool", bufs=1))

        def load(piece):
            b, kq = divmod(piece, PIECES_PER_B)
            raw = raw_pool.tile([P, PACK, M, RUN], BF16, name="raw")
            source = A[b].rearrange("(p j) m k r t -> p j m (k r t)", j=PACK)[
                :, :, :, kq * RUN : (kq + 1) * RUN
            ]
            if piece == 0:
                for m in range(M):
                    nc.sync.dma_start(out=raw[:, :, m], in_=source[:, :, m])
            else:
                nc.sync.dma_start(out=raw[:], in_=source)
            return raw

        def load_a5(b):
            a5_sb = a5_pool.tile([P, O_TILES * M * K * NT], BF16, name="a5_sb")
            nc.sync.dma_start(
                out=a5_sb[:].rearrange("o (ot x) -> o ot x", ot=O_TILES),
                in_=a5[b].rearrange("(ot o) m k t -> o ot (m k t)", o=P),
            )
            return a5_sb

        ctx.enter_context(tc.manual_schedule())

        setup = ctx.enter_context(tc.tile_pool(name="setup", bufs=1))
        once = ctx.enter_context(tc.tile_pool(name="once", bufs=1))
        rounds = ExitStack()
        twice = rounds.enter_context(tc.tile_pool(name="twice", bufs=2))
        thrice = rounds.enter_context(tc.tile_pool(name="thrice", bufs=3))
        reps = rounds.enter_context(tc.tile_pool(name="reps", bufs=REPS))
        kept = rounds.enter_context(tc.tile_pool(name="kept", bufs=KEPT))
        grouped_pairs = []
        for n in range(2):
            grouped_pair = kept.tile([P, 2, O * PACK], BF16, align_bytes=64, name="a_codes")
            grouped_pairs.append(grouped_pair)
        scaled_pair = kept.tile([P, 2, O * PACK], BF16, align_bytes=64, name="a_codes")
        gb_rows = setup.tile([P, P], BF16, name="gb_rows")
        nc.vector.memset(gb_rows[:], 0.0)
        ident_f32 = setup.tile([P, P], F32, name="ident_f32")
        make_identity(nc, ident_f32[:])

        w_rows = raw_pool.tile([P, len(weights), O_TILES, C], BF16, name="raw")

        def load_weight(n, name):
            nc.sync.dma_start(
                out=w_rows[:, n], in_=weights[name].rearrange("(ot o) c -> o ot c", o=P)
            )

        load_weight(0, "p1")
        first_raws = {0: load(0)}
        for n, name in enumerate(("p2", "p3", "p4")):
            load_weight(n + 1, name)
        first_raws[1] = load(1)
        nc.sync.dma_start(out=gb_rows[0:O_TILES, :], in_=gamma.rearrange("(ot o) -> ot o", o=P))
        nc.sync.dma_start(
            out=gb_rows[O_TILES : 2 * O_TILES, :], in_=beta.rearrange("(ot o) -> ot o", o=P)
        )
        first_a5 = load_a5(0)

        pool_ones = setup.tile([P, 2, POOLED], F32, name="pool_ones")
        nc.vector.tensor_reduce(
            out=pool_ones[:, 0, :],
            in_=ident_f32[:].rearrange("p (x t) -> p x t", t=NT),
            axis=AXIS_X,
            op=ALU.add,
        )
        nc.vector.tensor_reduce(
            out=pool_ones[:, 1, :].rearrange("p (k t) -> p k t", t=NT),
            in_=ident_f32[:].rearrange("p (k r t) -> p k t r", r=NR, t=NT),
            axis=AXIS_X,
            op=ALU.add,
        )
        nc.vector.tensor_scalar_mul(out=pool_mat[:, 0, :], in0=pool_ones[:, 0, :], scalar1=1.0 / NT)
        nc.vector.tensor_scalar_mul(out=pool_mat[:, 1, :], in0=pool_ones[:, 1, :], scalar1=1.0 / NR)

        grouped_w = {}

        def group_weight(n, name):
            words = w_rows[:, n].bitcast(F32).rearrange("o ot (p u) -> o ot u p", u=2)
            turned = psum_x.tile([P, O_TILES, 2, P], F32, name="acc")
            for ot in range(O_TILES):
                for u in range(2):
                    nc.tensor.transpose(turned[:, ot, u, :], words[:, ot, u, :], ident_f32[:])
            grouped = grouped_pairs[n // 2][:, n % 2, :]
            nc.scalar.copy(
                out=grouped.bitcast(F32).rearrange("p (ot o u) -> p ot o u", ot=O_TILES, u=2),
                in_=turned[:].rearrange("p ot u o -> p ot o u"),
            )
            grouped_w[name] = grouped

        def quantise_weight(i):
            name, factor = STATIONARY[i]
            scaled = grouped_w[name]
            if factor != 1.0:
                scaled = scaled_pair[:, i % 2, :]
                nc.vector.tensor_scalar_mul(out=scaled, in0=grouped_w[name], scalar1=factor)
            nc.vector.quantize_mx(
                out=w_codes[:, i, :].bitcast(FP8X4), scales=w_scales[:, i, :], in_=scaled
            )

        group_weight(0, "p1")
        for i in (W_A1_HI, W_A1_LO):
            quantise_weight(i)

        def finish_weights():
            for i in (W_A2, W_A3, W_A4):
                quantise_weight(i)

        def turn_gamma_beta():
            gb_turned = psum_small.tile([P, P], BF16, tag="small")
            nc.tensor.transpose(gb_turned[:], gb_rows[:], ident_bf16[:])
            nc.vector.tensor_copy(out=gamma_beta[:], in_=gb_turned[:, 0 : 2 * O_TILES])

        with rounds:

            def mix(acc, weight, ot, codes, scales, start, stop):
                nc.tensor.matmul_mx(
                    out=acc,
                    lhsT=w_codes[:, weight, ot * P : (ot + 1) * P].bitcast(FP8X4),
                    lhsT_scale=w_scales[:, weight, ot * P : (ot + 1) * P],
                    rhs=codes.bitcast(FP8X4),
                    rhs_scale=scales,
                    start=start,
                    stop=stop,
                )

            tiles = {("raw", piece): first_raws[piece] for piece in first_raws}
            tiles["a5", 0] = first_a5
            y_of = {(0, piece): y[:, piece, :] for piece in range(N_PIECES)}
            y_of.update({(1, piece): y[:, N_PIECES + piece, :] for piece in range(WHOLE)})

            def regroup_a_scalar(piece):
                raw = tiles["raw", piece]
                grouped_a = once.tile([P, COLS, PACK], BF16, align_bytes=64, name="grouped_a")
                split = KR * 5 // 16 if piece <= WHOLE + 1 else KR * 3 // 16
                target = grouped_a[:].rearrange("p (m th tl x) j -> p th m x j tl", m=M, tl=T_RUN, x=KR)
                source = raw[:].rearrange("p j m (x th tl) -> p th m x j tl", x=KR, tl=T_RUN)
                if piece == 0:
                    for m in range(M):
                        nc.scalar.copy(out=target[:, 1, m, split:], in_=source[:, 1, m, split:])
                else:
                    nc.scalar.copy(out=target[:, 1, :, split:], in_=source[:, 1, :, split:])
                tiles["grouped_a", piece] = grouped_a
                tiles["regroup_views", piece] = (target, source, split)

            def regroup_a_vector(piece):
                target, source, split = tiles["regroup_views", piece]
                if piece == 0:
                    for m in range(M):
                        nc.vector.tensor_copy(out=target[:, 0, m], in_=source[:, 0, m])
                        nc.vector.tensor_copy(out=target[:, 1, m, 0:split], in_=source[:, 1, m, 0:split])
                else:
                    nc.vector.tensor_copy(out=target[:, 0], in_=source[:, 0])
                    nc.vector.tensor_copy(out=target[:, 1, :, 0:split], in_=source[:, 1, :, 0:split])

            def sum_pairs_of_m(piece):
                by_m = tiles["grouped_a", piece][:].rearrange("p (m w) j -> p m (w j)", m=M)
                pair_sums = once.tile([P, 2, RUN * PACK], F32, name="pair_sums")
                nc.vector.tensor_add(out=pair_sums[:], in0=by_m[:, 0:2, :], in1=by_m[:, 2:4, :])
                tiles["pair_sums", piece] = pair_sums

            def quantise_a(piece):
                a_codes = kept.tile([P, COLS], U32, align_bytes=64, name="a_codes")
                a_scales = kept.tile([P, COLS], U8, align_bytes=64, name="a_scales")
                nc.vector.quantize_mx(
                    out=a_codes[:].bitcast(FP8X4),
                    scales=a_scales[:],
                    in_=tiles["grouped_a", piece][:].rearrange("p w j -> p (w j)"),
                )
                tiles["a_codes", piece], tiles["a_scales", piece] = a_codes, a_scales

            def finish_sum_over_m(piece):
                pair_sums = tiles["pair_sums", piece]
                grouped_small = tiles["grouped_small", piece]
                nc.vector.tensor_add(
                    out=grouped_small[:, 2 * SMALL * PACK :], in0=pair_sums[:, 0, :], in1=pair_sums[:, 1, :]
                )

            def turn(piece, j):
                raw = tiles["raw", piece]
                turned_ps = psum_turned.tile([P, M, HALVES, P], BF16, name="turned_ps")
                for m in range(M):
                    for h in range(HALVES):
                        nc.tensor.transpose(
                            turned_ps[:, m, h, :], raw[:, j, m, h * P : (h + 1) * P], ident_bf16[:]
                        )
                turned = thrice.tile([P, M, HALVES, P], BF16, name="turned")
                nc.scalar.copy(
                    out=turned[:].rearrange("p m h c -> p (m h c)").bitcast(F32),
                    in_=turned_ps[:].rearrange("p m h c -> p (m h c)").bitcast(F32),
                )
                tiles["turned", piece, j] = turned

            def pool(piece, j):
                if j == 0:
                    for i in range(M // 2):
                        tiles["pooled", piece, i] = psum_pooled.tile(
                            [P, 2, PACK, 2, HALVES, POOLED], F32, name="pooled%d" % i, tag="pooled"
                        )
                for m in range(M):
                    for h in range(HALVES):
                        nc.tensor.matmul(
                            out=tiles["pooled", piece, m // 2][:, :, j, m % 2, h, :],
                            lhsT=tiles["turned", piece, j][:, m, h, :],
                            rhs=pool_mat[:],
                            start=True,
                            stop=True,
                        )

            def round_means(piece):
                grouped_small = once.tile([P, SMALL_COLS * PACK], BF16, align_bytes=64, name="grouped_small")
                tiles["grouped_small", piece] = grouped_small
                grouped_tr = grouped_small[:, 0 : 2 * SMALL * PACK].rearrange(
                    "p (s w j) -> p s w j", s=2, j=PACK
                )
                for i in range(M // 2):
                    nc.scalar.copy(
                        out=grouped_tr[:, :, i * (SMALL // 2) : (i + 1) * (SMALL // 2), :],
                        in_=tiles["pooled", piece, i][:].rearrange("p s j m h x -> p s (m h x) j"),
                    )

            def quantise_means(piece):
                small_codes = kept.tile([P, SMALL_COLS], U32, align_bytes=64, name="small_codes")
                scales = small_scales[piece % KEPT]
                nc.vector.quantize_mx(
                    out=small_codes[:, 0 : 2 * SMALL].bitcast(FP8X4),
                    scales=scales[:, 0 : 2 * SMALL],
                    in_=tiles["grouped_small", piece][:, 0 : 2 * SMALL * PACK],
                )
                tiles["small_codes", piece] = small_codes

            def repeat_codes(piece):
                small_codes = tiles["small_codes", piece]
                at_rep_codes = reps.tile([P, COLS], U32, align_bytes=64, name="at_rep_codes")
                tiles["at_rep_codes", piece] = at_rep_codes
                for m in range(M):
                    nc.sync.dma_start(
                        out=at_rep_codes[:, m * RUN : (m + 1) * RUN]
                        .bitcast(I32)
                        .rearrange("p (t x) -> p t x", t=NT),
                        in_=small_codes[:, m * KR : (m + 1) * KR]
                        .bitcast(I32)
                        .unsqueeze(1)
                        .to_broadcast([P, NT, KR]),
                    )

            def repeat_codes_vector(piece):
                at_rep_codes = reps.tile([P, COLS], U32, align_bytes=64, name="at_rep_codes")
                nc.vector.tensor_copy(
                    out=at_rep_codes[:].bitcast(I32).rearrange("p (m t x) -> p m t x", m=M, t=NT),
                    in_=tiles["small_codes", piece][:, 0:SMALL]
                    .bitcast(I32)
                    .rearrange("p (m x) -> p m x", m=M)
                    .unsqueeze(2)
                    .to_broadcast([P, M, NT, KR]),
                )
                tiles["at_rep_codes", piece] = at_rep_codes

            def repeat_scales(piece):
                at_rep_scales = reps.tile([P, COLS], U8, align_bytes=64, name="at_rep_scales")
                tiles["at_rep_scales", piece] = at_rep_scales
                nc.vector.tensor_copy(
                    out=at_rep_scales[:].bitcast(I32).rearrange("p (m t x) -> p m t x", m=M, t=NT),
                    in_=small_scales[piece % KEPT][:, 0:SMALL]
                    .bitcast(I32)
                    .rearrange("p (m x) -> p m x", m=M)
                    .unsqueeze(2)
                    .to_broadcast([P, M, NT, KR // 4]),
                )

            def quantise_sum_over_m(piece):
                nc.vector.quantize_mx(
                    out=tiles["small_codes", piece][:, 2 * SMALL :].bitcast(FP8X4),
                    scales=small_scales[piece % KEPT][:, 2 * SMALL :],
                    in_=tiles["grouped_small", piece][:, 2 * SMALL * PACK :],
                )

            def mix_a4(pairs):
                a4_acc = psum_small.tile([P, len(pairs), SMALL], F32, tag="small", name="a4_acc")
                for n, (piece, ot) in enumerate(pairs):
                    mix(
                        a4_acc[:, n, :], W_A4, ot, tiles["small_codes", piece][:, SMALL : 2 * SMALL],
                        small_scales[piece % KEPT][:, SMALL : 2 * SMALL], True, True,
                    )
                    tiles["a4", piece, ot] = a4_acc[:, n : n + 1, :]
                if pairs == both_ots(pairs[0][0]):
                    tiles["a4", pairs[0][0]] = a4_acc[:]

            def both_ots(piece):
                return [(piece, ot) for ot in range(O_TILES)]

            def terms_without_r(piece, ots):
                b, kq = divmod(piece, PIECES_PER_B)
                n = len(ots)
                x_of_ot = M * K * NT
                a5_of_ots = tiles["a5", b][:, ots[0] * x_of_ot : (ots[0] + n) * x_of_ot]
                a4 = tiles["a4", piece] if n == O_TILES else tiles["a4", piece, ots[0]]
                no_r = twice.tile([P, n * M, NT * K_PIECE], F32, name="no_r")
                nc.vector.tensor_tensor(
                    out=no_r[:].rearrange("p g (t k) -> p g t k", t=NT),
                    in0=a4.rearrange("p n (m k t) -> p (n m) t k", k=K_PIECE, t=NT),
                    in1=a5_of_ots.rearrange(
                        "p (g kq k t) -> p kq g t k", kq=PIECES_PER_B, k=K_PIECE, t=NT
                    )[:, kq],
                    op=ALU.add,
                )
                for i, ot in enumerate(ots):
                    tiles["no_r", piece, ot] = no_r[:, i * M : (i + 1) * M, :]

            def mix_m(piece, ot, m):
                m_pair, i = divmod(m, 2)
                if ("acc", piece, ot, m_pair) not in tiles:
                    tiles["acc", piece, ot, m_pair] = psum_x.tile([P, 2, RUN], F32, name="acc")
                acc = tiles["acc", piece, ot, m_pair][:, i, :]
                cols = slice(m * RUN, (m + 1) * RUN)
                a_codes, a_scales = tiles["a_codes", piece][:, cols], tiles["a_scales", piece][:, cols]
                mix(acc, W_A1_HI, ot, a_codes, a_scales, True, False)
                mix(acc, W_A1_LO, ot, a_codes, a_scales, False, False)
                mix(
                    acc, W_A2, ot, tiles["small_codes", piece][:, 2 * SMALL :],
                    small_scales[piece % KEPT][:, 2 * SMALL :], False, False,
                )
                mix(
                    acc, W_A3, ot, tiles["at_rep_codes", piece][:, cols],
                    tiles["at_rep_scales", piece][:, cols], False, True,
                )

            def mix_pair(piece, ot, m_pair):
                if ("acc", piece, ot, m_pair) not in tiles:
                    tiles["acc", piece, ot, m_pair] = psum_x.tile([P, 2, RUN], F32, name="acc")
                acc = tiles["acc", piece, ot, m_pair]
                bank = acc[:].rearrange("p i x -> p (i x)")
                cols = slice(2 * m_pair * RUN, (2 * m_pair + 2) * RUN)
                a_codes, a_scales = tiles["a_codes", piece][:, cols], tiles["a_scales", piece][:, cols]
                mix(bank, W_A1_HI, ot, a_codes, a_scales, True, False)
                mix(bank, W_A1_LO, ot, a_codes, a_scales, False, False)
                for i in range(2):
                    mix(
                        acc[:, i, :], W_A2, ot, tiles["small_codes", piece][:, 2 * SMALL :],
                        small_scales[piece % KEPT][:, 2 * SMALL :], False, False,
                    )
                mix(
                    bank, W_A3, ot, tiles["at_rep_codes", piece][:, cols],
                    tiles["at_rep_scales", piece][:, cols], False, True,
                )

            def mix_pair_early(piece, m_pair):
                if m_pair == 0:
                    bank = psum_turned.tile([P, 2, RUN], F32, name="turned_ps")
                else:
                    bank = psum_pooled.tile([P, 2, RUN], F32, name="bank", tag="pooled")
                tiles["acc", piece, 1, m_pair] = bank
                mix_pair(piece, 1, m_pair)

            def add_out(piece, ot, m_pair):
                acc = tiles["acc", piece, ot, m_pair]
                nc.vector.scalar_tensor_tensor(
                    out=y_of[ot, piece][:, 2 * m_pair * RUN : (2 * m_pair + 2) * RUN].rearrange(
                        "p (x r) -> p x r", r=NR
                    ),
                    in0=tiles["no_r", piece, ot][:, 2 * m_pair : 2 * m_pair + 2, :]
                    .rearrange("p g x -> p (g x)")
                    .unsqueeze(2)
                    .to_broadcast([P, 2 * NT * K_PIECE, NR]),
                    scalar=2.0 * UP,
                    in1=acc[:].rearrange("p i (x r) -> p (i x) r", r=NR),
                    op0=ALU.mult,
                    op1=ALU.add,
                )

            def relu(piece, ot):
                nc.scalar.activation(
                    out=y_of[ot, piece], in_=y_of[ot, piece], func=ACT.Relu,
                    accum_out=sums[:, ot, piece : piece + 1],
                )

            def square(piece, ot):
                squared = once.tile([P, COLS], BF16, name="squared")
                nc.scalar.activation(
                    out=squared[:], in_=y_of[ot, piece], func=ACT.Square,
                    accum_out=squares[:, ot, piece : piece + 1],
                )

            def last_half(piece, ot, half):
                col = (piece, N_PIECES)[half]
                part = y_of[ot, piece][:, half * 2 * RUN : (half + 1) * 2 * RUN]
                return part, sums[:, ot, col : col + 1], squares[:, ot, col : col + 1]

            def last_relu(piece, ot, half):
                part, sum_col, square_col = last_half(piece, ot, half)
                nc.vector.tensor_scalar(
                    out=part, in0=part, scalar1=0.0, scalar2=0.0, op0=ALU.max, op1=ALU.add,
                    accum_out=sum_col,
                )

            def last_square(piece, ot, half):
                part, sum_col, square_col = last_half(piece, ot, half)
                squared = once.tile([P, COLS], BF16, name="squared")
                nc.scalar.activation(
                    out=squared[:, 0 : 2 * RUN], in_=part, func=ACT.Square, accum_out=square_col
                )

            assert PACK == M == O_TILES * (M // 2)
            LAST = PACK - 1

            def ots_in_round(piece):
                return range(O_TILES) if piece < WHOLE else range(1)

            def multiply(piece, unit):
                if piece < WHOLE:
                    mix_pair(piece, *divmod(unit, M // 2))
                else:
                    mix_m(piece, 0, unit)

            def empty(piece, unit):
                if piece < WHOLE:
                    add_out(piece, *divmod(unit, M // 2))
                elif unit % 2 == 1:
                    add_out(piece, 0, unit // 2)

            regroup_a_scalar(0)
            turn(0, 0)
            turn(0, 1)
            group_weight(1, "p2")
            group_weight(2, "p3")
            pool(0, 0)
            turn(0, 2)
            pool(0, 1)
            turn(0, 3)
            pool(0, 2)
            group_weight(3, "p4")
            tiles["raw", 2] = load(2)
            final = N_PIECES - 1
            order = EARLY + (final,) + ANEW
            for i in range(-1, N_PIECES):
                ahead, here, behind = i + 1, i, i - 1
                prepares = ahead < N_PIECES
                turns_next = ahead + 1 < N_PIECES
                multiplies = here >= 0
                finishes = behind >= 0
                both = 0 <= behind < WHOLE
                if 3 <= ahead + 2 < N_PIECES:
                    tiles["raw", ahead + 2] = load(ahead + 2)
                if finishes:
                    empty(behind, LAST)
                if here == final:
                    mix_a4([(final, 0)] + [(piece, 1) for piece in order[:3]])
                elif multiplies:
                    mix_a4([(here, ot) for ot in ots_in_round(here)])
                if multiplies:
                    terms_without_r(here, ots_in_round(here))
                if ahead == PIECES_PER_B:
                    tiles["a5", 1] = load_a5(1)
                if here == final:
                    for piece in ANEW[: len(EARLY)]:
                        repeat_scales(piece)
                if 0 < ahead < N_PIECES:
                    regroup_a_scalar(ahead)
                if turns_next:
                    turn(ahead + 1, 0)
                if prepares:
                    pool(ahead, 3)
                    round_means(ahead)
                    regroup_a_vector(ahead)
                if multiplies:
                    multiply(here, 0)
                    empty(here, 0)
                if finishes:
                    relu(behind, 0)
                if turns_next:
                    turn(ahead + 1, 1)
                    pool(ahead + 1, 0)
                if prepares:
                    sum_pairs_of_m(ahead)
                if 0 < ahead < N_PIECES:
                    quantise_means(ahead)
                    repeat_codes(ahead)
                if ahead == 0:
                    finish_weights()
                if ahead == 2:
                    turn_gamma_beta()
                if multiplies:
                    multiply(here, 1)
                    empty(here, 1)
                if both:
                    square(behind, 0)
                    relu(behind, 1)
                if turns_next:
                    turn(ahead + 1, 2)
                    pool(ahead + 1, 1)
                if ahead == 0:
                    quantise_means(ahead)
                    repeat_codes(ahead)
                if prepares:
                    finish_sum_over_m(ahead)
                    quantise_a(ahead)
                    quantise_sum_over_m(ahead)
                    repeat_scales(ahead)
                if multiplies:
                    multiply(here, 2)
                if multiplies and here < final:
                    empty(here, 2)
                if both:
                    square(behind, 1)
                elif finishes:
                    square(behind, 0)
                if turns_next:
                    turn(ahead + 1, 3)
                    pool(ahead + 1, 2)
                if multiplies:
                    multiply(here, LAST)
                if here == final - 1:
                    for piece in EARLY:
                        for m_pair in range(M // 2):
                            mix_pair_early(piece, m_pair)
                    for piece in ANEW[: len(EARLY)]:
                        repeat_codes(piece)

            count = float(B * POSITIONS)
            total = keep.tile([P, O_TILES], F32)
            total_sq = keep.tile([P, O_TILES], F32)
            minus_mean = keep.tile([P, O_TILES], F32)
            mean_sq = keep.tile([P, O_TILES], F32)
            var = keep.tile([P, O_TILES], F32)
            std = keep.tile([P, O_TILES], F32)
            gain = keep.tile([P, O_TILES], F32)
            shift = keep.tile([P, O_TILES], F32)

            def variance(ot):
                col = slice(ot, ot + 1)
                nc.vector.tensor_reduce(out=total[:, col], in_=sums[:, ot, :], axis=AXIS_X, op=ALU.add)
                nc.vector.tensor_scalar_mul(out=minus_mean[:, col], in0=total[:, col], scalar1=-1.0 / count)
                nc.vector.tensor_mul(out=mean_sq[:, col], in0=minus_mean[:, col], in1=minus_mean[:, col])
                nc.vector.tensor_reduce(out=total_sq[:, col], in_=squares[:, ot, :], axis=AXIS_X, op=ALU.add)
                nc.vector.scalar_tensor_tensor(
                    out=var[:, col], in0=total_sq[:, col], scalar=1.0 / count, in1=mean_sq[:, col],
                    op0=ALU.mult, op1=ALU.subtract,
                )
                nc.vector.tensor_scalar(
                    out=var[:, col], in0=var[:, col], scalar1=0.0, scalar2=BN_EPS * UP * UP,
                    op0=ALU.max, op1=ALU.add,
                )
                nc.scalar.sqrt(out=std[:, col], in_=var[:, col])

            def gain_and_shift(ot):
                col = slice(ot, ot + 1)
                nc.vector.reciprocal(out=gain[:, col], in_=std[:, col])
                nc.vector.tensor_mul(out=gain[:, col], in0=gain[:, col], in1=gamma_beta[:, col])
                nc.vector.scalar_tensor_tensor(
                    out=shift[:, col], in0=gain[:, col], scalar=minus_mean[:, col],
                    in1=gamma_beta[:, O_TILES + ot : O_TILES + ot + 1], op0=ALU.mult, op1=ALU.add,
                )

            def normalise(ot, step, staged, groups, engine):
                b, m = divmod(step, M)
                stored = 0
                for view, first in groups:
                    n = view.shape[1]
                    q = first - b * PIECES_PER_B
                    source = view[:, :, m * RUN : (m + 1) * RUN].rearrange(
                        "p q (th tl x) -> p th q x tl", tl=T_RUN, x=KR
                    )
                    target = staged[:, q : q + n].rearrange("p q x (th tl) -> p th q x tl", tl=T_RUN)
                    for th in range(NT // T_RUN):
                        if engine is not nc.scalar:
                            engine.tensor_scalar(
                                out=target[:, th], in0=source[:, th], scalar1=gain[:, ot : ot + 1],
                                scalar2=shift[:, ot : ot + 1], op0=ALU.mult, op1=ALU.add,
                            )
                        else:
                            nc.scalar.activation(
                                out=target[:, th], in_=source[:, th], func=ACT.Identity,
                                bias=shift[:, ot : ot + 1], scale=gain[:, ot : ot + 1],
                            )
                    done = q + n
                    if step == 0 and ot == 0 or done == PIECES_PER_B:
                        nc.sync.dma_start(
                            out=out[b].rearrange("(ot o) m k r t -> o ot m (k r t)", o=P)[
                                :, ot, m, stored * RUN : done * RUN
                            ],
                            in_=staged[:, stored:done].rearrange("p q x t -> p (q x t)"),
                        )
                        stored = done

            def normalise_0(step, engine):
                first = step // M * PIECES_PER_B
                n = PIECES_PER_B // 2 if step == 0 else PIECES_PER_B
                normalise(
                    0, step, raw_pool.tile([P, PIECES_PER_B, KR, NT], F32, name="raw"),
                    [(y[:, q : q + n, :], q) for q in range(first, first + PIECES_PER_B, n)], engine,
                )

            late_a = once.tile([P, 2, COLS], F32, align_bytes=64, name="grouped_a")
            late_b = once.tile([P, 2, COLS], F32, name="pair_sums")
            late_groups = [(y[:, 0:2, :], WHOLE), (late_b[:], WHOLE + 2), (late_a[:], WHOLE + 4)]
            for view, first in late_groups:
                for n in range(2):
                    y_of[1, first + n] = view[:, n, :]

            terms_without_r(order[0], range(1, 2))
            last_relu(final, 0, 0)
            last_square(final, 0, 0)
            add_out(final, 0, 1)
            terms_without_r(order[1], range(1, 2))
            last_relu(final, 0, 1)
            last_square(final, 0, 1)
            for n, piece in enumerate(order):
                last = n == LATE - 1
                if piece not in EARLY:
                    mix_pair(piece, 1, 0)
                    mix_pair(piece, 1, 1)
                add_out(piece, 1, 0)
                if n == 2:
                    mix_a4([(late, 1) for late in order[3:]])
                if 0 < n < LATE - 1:
                    terms_without_r(order[n + 1], range(1, 2))
                if n == 0:
                    variance(0)
                    add_out(piece, 1, 1)
                    gain_and_shift(0)
                if n == 0:
                    normalise_0(0, nc.vector)
                    normalise_0(1, nc.scalar)
                else:
                    normalise_0(n + 1, nc.gpsimd if n == 3 else nc.vector)
                if n > 0:
                    add_out(piece, 1, 1)
                if piece == final:
                    repeat_codes_vector(ANEW[-1])
                    repeat_scales(ANEW[-1])
                if last:
                    for half in range(2):
                        last_relu(piece, 1, half)
                        last_square(piece, 1, half)
                    normalise_0(n + 2, nc.vector)
                else:
                    relu(piece, 1)
                    square(piece, 1)
            variance(1)
            gain_and_shift(1)

        staged_pool = ctx.enter_context(tc.tile_pool(name="staged_pool", bufs=4))
        whole_groups = [
            [(y[:, N_PIECES : N_PIECES + PIECES_PER_B, :], 0)],
            [(y[:, N_PIECES + PIECES_PER_B :, :], PIECES_PER_B)] + late_groups,
        ]
        for step in range(B * M):
            staged = staged_pool.tile([P, PIECES_PER_B, KR, NT], F32)
            normalise(1, step, staged, whole_groups[step // M], nc.vector if step % 2 == 0 else nc.scalar)
